import numpy as np
import ml_dtypes


def mxq(x, axis, fmt="e4m3"):
    dtype, down = {"e4m3": (ml_dtypes.float8_e4m3fn, 7), "e5m2": (ml_dtypes.float8_e5m2, 14)}[fmt]
    v = np.moveaxis(np.asarray(x, np.float32).astype(ml_dtypes.bfloat16).astype(np.float64), axis, -1)
    blocks = v.reshape(v.shape[:-1] + (-1, 32))
    amax = np.abs(blocks).max(-1, keepdims=True)
    byte = np.maximum(np.where(amax > 0, np.frexp(amax)[1] - 1 + 127, 0) - down, 1)
    scale = np.exp2(byte - 127.0)
    codes = (blocks / scale).astype(np.float32).astype(dtype).astype(np.float64)
    return np.moveaxis((codes * scale).reshape(v.shape), -1, axis)


WIDE = False


def mx_kscale(k):
    if not WIDE:
        return np.ones(k)
    levels = np.array([10, -10, 5, -5, 0])
    if k % 512:
        return np.exp2(np.random.permutation(np.resize(levels, k // 32))).repeat(32)
    a = np.empty((k // 512, 16))
    for p in range(k // 512):
        a[p, :8] = np.random.permutation(np.resize(levels, 8))
        for g in range(8):
            far = levels[np.abs(levels - a[p, g]) >= 10]
            a[p, g + 8] = far[np.random.randint(len(far))]
    return np.exp2(a.ravel()).repeat(32)


BF16 = ml_dtypes.bfloat16


def bf(x):
    return np.asarray(x, np.float32).astype(BF16)


def f64(x):
    return np.asarray(x).astype(np.float64)


N, C_IN, C_OUT, C_DGRAM, C_AA, C_ESM = 128, 512, 128, 39, 22, 1280
LN_EPS = 1e-5


def layer_norm(x, g, b):
    mu = x.mean(-1, keepdims=True)
    var = x.var(-1, keepdims=True)
    return (x - mu) * (1.0 / np.sqrt(var + LN_EPS)) * g + b


def setup_inputs():
    rn, ru = np.random.standard_normal, np.random.uniform
    s = mx_kscale(C_IN)

    def vec():
        return bf(rn(C_OUT) * 0.1)

    def row():
        return bf(rn(C_OUT)[None, :])

    return {
        "act_dgram": bf(rn((N, N, C_OUT)) * 0.2),
        "aa_proj1": bf(rn((N, C_OUT)) * 0.6),
        "aa_proj2": bf(rn((N, C_OUT)) * 0.6),
        "esm_proj1": bf(rn((N, C_OUT))),
        "esm_proj2": bf(rn((N, C_OUT))),
        "query_embedding": bf(rn((N, N, C_IN)) * (0.5 + 1.5 * ru(size=(N, N)))[..., None] + rn((N, N))[..., None]),
        "pseudo_beta_mask": bf(ru(size=N)),
        "backbone_mask": bf(ru(size=N)),
        "multichain_mask_2d": bf(ru(size=(N, N))),
        "unit_x": bf(rn((N, N))),
        "unit_y": bf(rn((N, N))),
        "unit_z": bf(rn((N, N))),
        "ln_g": bf((1.0 + 0.1 * rn(C_IN)) * s),
        "ln_b": bf(0.1 * rn(C_IN) * s),
        "w_q": bf(rn((C_IN, C_OUT)) / np.sqrt(C_IN) / s[:, None]),
        "b_q": vec(),
        "w_pbm": row(), "b_pbm": vec(),
        "w_x": row(), "b_x": vec(),
        "w_y": row(), "b_y": vec(),
        "w_z": row(), "b_z": vec(),
        "w_bb": row(), "b_bb": vec(),
    }


def reference(act_dgram, aa_proj1, aa_proj2, esm_proj1, esm_proj2, query_embedding,
              pseudo_beta_mask, backbone_mask, multichain_mask_2d, unit_x, unit_y, unit_z,
              ln_g, ln_b, w_q, b_q, w_pbm, b_pbm, w_x, b_x, w_y, b_y, w_z, b_z, w_bb, b_bb):
    pbm, bbm, mc = f64(pseudo_beta_mask), f64(backbone_mask), f64(multichain_mask_2d)
    pb2 = pbm[:, None] * pbm[None, :] * mc
    bb2 = bbm[:, None] * bbm[None, :] * mc
    act = f64(act_dgram)
    act = act + (pb2[..., None] * f64(w_pbm)[0] + f64(b_pbm))
    act = act + f64(aa_proj1)[None, :, :]
    act = act + f64(aa_proj2)[:, None, :]
    act = act + ((f64(unit_x) * bb2)[..., None] * f64(w_x)[0] + f64(b_x))
    act = act + ((f64(unit_y) * bb2)[..., None] * f64(w_y)[0] + f64(b_y))
    act = act + ((f64(unit_z) * bb2)[..., None] * f64(w_z)[0] + f64(b_z))
    act = act + (bb2[..., None] * f64(w_bb)[0] + f64(b_bb))
    act = act + f64(esm_proj1)[None, :, :]
    act = act + f64(esm_proj2)[:, None, :]
    q = layer_norm(f64(query_embedding), f64(ln_g), f64(ln_b))
    act = act + (mxq(q, 2, "e4m3") @ mxq(f64(w_q), 0, "e4m3")) + f64(b_q)
    return act

@@ -1,0 +1,325 @@
+from contextlib import ExitStack
+
+import concourse.mybir as mybir
+from concourse.masks import make_identity
+
+F32 = mybir.dt.float32
+BF16 = mybir.dt.bfloat16
+U32 = mybir.dt.uint32
+U8 = mybir.dt.uint8
+FP8X4 = mybir.dt.float8_e4m3fn_x4
+ALU = mybir.AluOpType
+ACT = mybir.ActivationFunctionType
+
+P = 128
+C_IN = 512
+PACK = 4
+LN_EPS = 1e-5
+GROUP = 4
+PAIRS = GROUP * P
+N_GROUPS = P // GROUP
+N_FEAT = 5
+X_AHEAD = 4
+VECTOR_COLUMNS = 2
+GPSIMD_PAIRS = 3 * PAIRS // 4
+
+ROW_W = 0
+ROW_PBM = 5
+ROW_BBM = 6
+ROW_BIAS = 7
+N_ROWS = 13
+
+LAG_NORMALISE = 2
+LAG_TRANSPOSE = 3
+LAG_REGROUP = 4
+LAG_PROJECT = 5
+LAG_TURN_BACK = 6
+LAG_STORE = 7
+N_STEPS = N_GROUPS + LAG_STORE
+
+FLOPS = 2 * P * P * C_IN * P
+
+
+def as_row(vector):
+    return vector.rearrange("(o c) -> o c", o=1)
+
+
+def tile_templatepairembeddermultimer_pa_kernel(
+    tc,
+    act_dgram, aa_proj1, aa_proj2, esm_proj1, esm_proj2, query_embedding,
+    pseudo_beta_mask, backbone_mask, multichain_mask_2d, unit_x, unit_y, unit_z,
+    ln_g, ln_b, w_q, b_q, w_pbm, b_pbm, w_x, b_x, w_y, b_y, w_z, b_z, w_bb, b_bb,
+    out,
+):
+    nc = tc.nc
+    with ExitStack() as stack:
+        stack.enter_context(tc.manual_schedule())
+        keep = stack.enter_context(tc.tile_pool(name="keep", bufs=1))
+        x_pool = stack.enter_context(tc.tile_pool(name="x", bufs=X_AHEAD + LAG_NORMALISE + 1))
+        act_pool = stack.enter_context(tc.tile_pool(name="act", bufs=LAG_TURN_BACK + 2))
+        stat_pool = stack.enter_context(tc.tile_pool(name="stat", bufs=4))
+        work = stack.enter_context(tc.tile_pool(name="work", bufs=3))
+        scrap = stack.enter_context(tc.tile_pool(name="scrap", bufs=4))
+        psum_keep = stack.enter_context(tc.psum_pool(name="psum_keep", bufs=1))
+        psum_y = stack.enter_context(tc.psum_pool(name="psum_y", bufs=PACK))
+
+        x_tiles, act_tiles, vector_stats, neg_means, stds, rstds, y_tiles, y_banks, plane_tiles = (
+            {}, {}, {}, {}, {}, {}, {}, {}, {})
+        grouped_tiles, code_tiles, proj_banks, proj_tiles, res_tiles, bases = {}, {}, {}, {}, {}, {}
+
+        def columns_of(g):
+            return slice(g * GROUP, (g + 1) * GROUP)
+
+        def load_x(g):
+            x_tiles[g] = x_pool.tile([P, GROUP, C_IN], BF16, name="x_g")
+            nc.sync.dma_start(out=x_tiles[g][:], in_=query_embedding[:, columns_of(g), :])
+
+        def load_act(g):
+            act_tiles[g] = act_pool.tile([P, GROUP, P], BF16, name="act_g")
+            nc.sync.dma_start(out=act_tiles[g][:], in_=act_dgram[:, columns_of(g), :])
+
+        def vector_statistics(g):
+            vector_stats[g] = stat_pool.tile([P, VECTOR_COLUMNS, 2], F32, name="mean_var")
+            for jj in range(VECTOR_COLUMNS):
+                partial = stat_pool.tile([P, 6], F32, name="partial")
+                nc.vector.bn_stats(out=partial[:], in_=x_tiles[g][:, jj, :])
+                nc.vector.bn_aggr(out=vector_stats[g][:, jj, :], in_=partial[:])
+
+        def scalar_statistics(g):
+            neg_means[g] = stat_pool.tile([P, GROUP], F32, name="neg_mean")
+            stds[g] = stat_pool.tile([P, GROUP], F32, name="std")
+            row_sum = stat_pool.tile([P, GROUP - VECTOR_COLUMNS], F32, name="row_sum")
+            dev_sq = stat_pool.tile([P, GROUP - VECTOR_COLUMNS], F32, name="dev_sq")
+            for jj in range(VECTOR_COLUMNS, GROUP):
+                unread = scrap.tile([P, C_IN], BF16, name="unread")
+                nc.scalar.activation(
+                    out=unread[:], in_=x_tiles[g][:, jj, :], func=ACT.Identity,
+                    accum_out=row_sum[:, jj - VECTOR_COLUMNS : jj - VECTOR_COLUMNS + 1])
+            nc.scalar.mul(out=neg_means[g][:, VECTOR_COLUMNS:], in_=row_sum[:], mul=-1.0 / C_IN)
+            if g > 0:
+                finish_vector_statistics(g - 1)
+            for jj in range(VECTOR_COLUMNS, GROUP):
+                unread = scrap.tile([P, C_IN], BF16, name="unread")
+                nc.scalar.activation(
+                    out=unread[:], in_=x_tiles[g][:, jj, :], func=ACT.Square, bias=neg_means[g][:, jj : jj + 1],
+                    scale=1.0, accum_out=dev_sq[:, jj - VECTOR_COLUMNS : jj - VECTOR_COLUMNS + 1])
+            nc.scalar.activation(
+                out=stds[g][:, VECTOR_COLUMNS:], in_=dev_sq[:], func=ACT.Sqrt, bias=eps[:, 0:1], scale=1.0 / C_IN)
+
+        def finish_vector_statistics(g):
+            nc.scalar.mul(out=neg_means[g][:, 0:VECTOR_COLUMNS], in_=vector_stats[g][:, :, 0], mul=-1.0)
+            nc.scalar.activation(
+                out=stds[g][:, 0:VECTOR_COLUMNS], in_=vector_stats[g][:, :, 1], func=ACT.Sqrt, bias=eps[:, 0:1], scale=1.0)
+
+        def inverse_std(g):
+            rstds[g] = stat_pool.tile([P, GROUP], F32, name="rstd")
+            nc.vector.reciprocal(out=rstds[g][:], in_=stds[g][:])
+
+        def normalise(g):
+            y_tiles[g] = work.tile([P, GROUP, C_IN], F32, name="y_g")
+            for jj in range(GROUP):
+                nc.gpsimd.tensor_scalar(
+                    out=y_tiles[g][:, jj, :], in0=x_tiles[g][:, jj, :],
+                    scalar1=neg_means[g][:, jj : jj + 1], scalar2=rstds[g][:, jj : jj + 1], op0=ALU.add, op1=ALU.mult)
+
+        def transpose(g):
+            y_banks[g] = []
+            for t in range(PACK):
+                y_t = psum_y.tile([P, GROUP, P], F32, name="y_t")
+                for jj in range(GROUP):
+                    nc.tensor.transpose(y_t[:, jj, :], y_tiles[g][:, jj, t:C_IN:PACK], ident_f[:])
+                y_banks[g].append(y_t)
+
+        def gain_shift(g):
+            plane_tiles[g] = work.tile([P, PACK, PAIRS], BF16, name="q_planes")
+            for t in range(PACK):
+                nc.scalar.activation(
+                    out=plane_tiles[g][:, t, :], in_=y_banks[g][t][:].rearrange("p a b -> p (a b)"), func=ACT.Identity,
+                    scale=gain[:, t : t + 1], bias=shift[:, t : t + 1])
+
+        def regroup(g):
+            q_planes = plane_tiles[g]
+            q_grouped = work.tile([P, PAIRS, PACK], BF16, name="q_grouped", align_bytes=64)
+            grouped_tiles[g] = q_grouped
+            nc.gpsimd.tensor_scalar(
+                out=q_grouped[:, 0:GPSIMD_PAIRS, :], in0=q_planes[:, :, 0:GPSIMD_PAIRS].rearrange("p t r -> p r t"),
+                scalar1=1.0, scalar2=0.0, op0=ALU.mult, op1=ALU.add)
+            nc.scalar.copy(
+                out=q_grouped[:, GPSIMD_PAIRS:, :].rearrange("p (c i) t -> p c t i", i=4),
+                in_=q_planes[:, :, GPSIMD_PAIRS:].rearrange("p t (c i) -> p c t i", i=4))
+
+        def quantise(g):
+            q_codes = work.tile([P, PAIRS], U32, name="q_codes", align_bytes=64)
+            q_scales = work.tile([P, PAIRS], U8, name="q_scales", align_bytes=64)
+            nc.vector.quantize_mx(
+                out=q_codes[:].bitcast(FP8X4), scales=q_scales[:], in_=grouped_tiles[g][:].rearrange("p r t -> p (r t)"))
+            code_tiles[g] = (q_codes, q_scales)
+
+        def project(g):
+            q_codes, q_scales = code_tiles[g]
+            proj_banks[g] = psum_mx.tile([P, PAIRS], F32, name="proj_ps")
+            nc.tensor.matmul_mx(
+                out=proj_banks[g][:],
+                lhsT=w_codes[:].bitcast(FP8X4), lhsT_scale=w_scales[:],
+                rhs=q_codes[:].bitcast(FP8X4), rhs_scale=q_scales[:],
+                start=True, stop=True)
+
+        def copy_out(g):
+            proj_tiles[g] = work.tile([P, GROUP, P], F32, name="proj_t")
+            nc.scalar.copy(out=proj_tiles[g][:].rearrange("p a b -> p (a b)"), in_=proj_banks[g][:])
+
+        def turn_back(g):
+            base = psum_base.tile([P, GROUP, P], F32, name="base")
+            bases[g] = base
+            for jj in range(GROUP):
+                j = g * GROUP + jj
+                nc.tensor.matmul(out=base[:, jj, :], lhsT=col_term_t[:], rhs=ident_f[:], is_transpose=True,
+                                 start=True, stop=False)
+                nc.tensor.matmul(out=base[:, jj, :], lhsT=row_term_t[:, j : j + 1].to_broadcast([P, P]), rhs=ident_f[:],
+                                 is_transpose=True, start=False, stop=False)
+                nc.tensor.matmul(out=base[:, jj, :], lhsT=proj_tiles[g][:, jj, :], rhs=ident_f[:], is_transpose=True,
+                                 start=False, stop=True)
+
+        def rank_one(g):
+            res_tiles[g] = work.tile([P, GROUP, P], F32, name="res")
+            for m in range(N_FEAT):
+                for jj in range(GROUP):
+                    j = g * GROUP + jj
+                    nc.vector.scalar_tensor_tensor(
+                        out=res_tiles[g][:, jj, :], in0=w_spread[m], scalar=feat[:, m, j : j + 1],
+                        in1=act_tiles[g][:, jj, :] if m == 0 else res_tiles[g][:, jj, :], op0=ALU.mult, op1=ALU.add)
+
+        def add_store(g):
+            nc.vector.tensor_tensor(out=res_tiles[g][:], in0=res_tiles[g][:], in1=bases[g][:], op=ALU.add)
+            nc.sync.dma_start(out=out[:, columns_of(g), :], in_=res_tiles[g][:])
+
+        def in_range(g):
+            return 0 <= g < N_GROUPS
+
+        def step(s):
+            if in_range(s + X_AHEAD):
+                load_x(s + X_AHEAD)
+            if in_range(s):
+                load_act(s)
+            if in_range(s - LAG_PROJECT):
+                quantise(s - LAG_PROJECT)
+            if in_range(s - LAG_STORE):
+                add_store(s - LAG_STORE)
+            if in_range(s - LAG_REGROUP):
+                regroup(s - LAG_REGROUP)
+            if in_range(s - LAG_NORMALISE):
+                inverse_std(s - LAG_NORMALISE)
+                normalise(s - LAG_NORMALISE)
+            if in_range(s - LAG_TRANSPOSE):
+                transpose(s - LAG_TRANSPOSE)
+            if in_range(s - LAG_PROJECT):
+                project(s - LAG_PROJECT)
+            if in_range(s - LAG_TURN_BACK):
+                turn_back(s - LAG_TURN_BACK)
+            if in_range(s):
+                vector_statistics(s)
+                scalar_statistics(s)
+            if s == N_GROUPS:
+                finish_vector_statistics(N_GROUPS - 1)
+            if in_range(s - LAG_TRANSPOSE):
+                gain_shift(s - LAG_TRANSPOSE)
+            if in_range(s - LAG_PROJECT):
+                copy_out(s - LAG_PROJECT)
+            if in_range(s - LAG_TURN_BACK):
+                rank_one(s - LAG_TURN_BACK)
+
+        eps = keep.tile([P, 1], F32, name="eps")
+        nc.vector.memset(eps[:], LN_EPS)
+        rows = keep.tile([P, P], BF16, name="rows")
+        nc.vector.memset(rows[:], 0.0)
+        table_warm = keep.tile([P, 1], F32, name="table_warm")
+        nc.scalar.activation(out=table_warm[:], in_=eps[:], func=ACT.Sqrt)
+        ident_f = keep.tile([P, P], F32, name="ident_f")
+        make_identity(nc, ident_f[:])
+        ident_b = keep.tile([P, P], BF16, name="ident_b")
+        make_identity(nc, ident_b[:])
+
+        load_x(0)
+        load_x(1)
+        gain_in = keep.tile([P, PACK], BF16, name="gain_in")
+        nc.sync.dma_start(out=gain_in[:], in_=ln_g.rearrange("(p t) -> p t", t=PACK))
+        shift_in = keep.tile([P, PACK], BF16, name="shift_in")
+        nc.sync.dma_start(out=shift_in[:], in_=ln_b.rearrange("(p t) -> p t", t=PACK))
+        for n, row in enumerate((w_pbm, w_x, w_y, w_z, w_bb, as_row(pseudo_beta_mask), as_row(backbone_mask))):
+            nc.sync.dma_start(out=rows[ROW_W + n : ROW_W + n + 1, :], in_=row)
+        load_x(2)
+        for n, vector in enumerate((b_q, b_pbm, b_x, b_y, b_z, b_bb)):
+            nc.sync.dma_start(out=rows[ROW_BIAS + n : ROW_BIAS + n + 1, :], in_=as_row(vector))
+        w_planes = keep.tile([P, PACK, P], BF16, name="w_planes")
+        nc.sync.dma_start(out=w_planes[:], in_=w_q.rearrange("(p t) c -> p t c", t=PACK))
+        load_x(3)
+        small = {}
+        for name, matrix in (
+            ("mc", multichain_mask_2d), ("ux", unit_x), ("uy", unit_y), ("uz", unit_z),
+            ("aa1", aa_proj1), ("esm1", esm_proj1), ("aa2", aa_proj2), ("esm2", esm_proj2),
+        ):
+            small[name] = keep.tile([P, P], BF16, name="in_" + name)
+            nc.sync.dma_start(out=small[name][:], in_=matrix)
+
+        for s in range(LAG_TRANSPOSE):
+            step(s)
+
+        gain = keep.tile([P, PACK], F32, name="gain")
+        nc.vector.tensor_copy(out=gain[:], in_=gain_in[:])
+        shift = keep.tile([P, PACK], F32, name="shift")
+        nc.vector.tensor_copy(out=shift[:], in_=shift_in[:])
+        columns = keep.tile([P, N_ROWS], F32, name="columns")
+        bias_total = keep.tile([P, 1], F32, name="bias_total")
+        row_term_t = keep.tile([P, P], F32, name="row_term_t")
+        col_term_t = keep.tile([P, P], F32, name="col_term_t")
+        feat = keep.tile([P, N_FEAT, P], F32, name="feat")
+        spread_a = psum_keep.tile([P, 4, P], F32, name="spread_a")
+        spread_b = psum_keep.tile([P, 3, P], F32, name="spread_b")
+
+        def spread(dst, row):
+            nc.tensor.transpose(dst, columns[:, row : row + 1].to_broadcast([P, P]), ident_f[:])
+
+        with tc.psum_pool(name="psum_setup", bufs=1) as psum_setup:
+            rows_t = psum_setup.tile([P, P], BF16, name="rows_t")
+            nc.tensor.transpose(rows_t[:], rows[:], ident_b[:])
+            nc.vector.tensor_copy(out=columns[:], in_=rows_t[:, 0:N_ROWS])
+            for m in range(4):
+                spread(spread_a[:, m, :], ROW_W + m)
+            spread(spread_b[:, 0, :], ROW_W + 4)
+            spread(spread_b[:, 1, :], ROW_PBM)
+            spread(spread_b[:, 2, :], ROW_BBM)
+            w_spread = [spread_a[:, m, :] for m in range(4)] + [spread_b[:, 0, :]]
+            nc.vector.reduce_sum(out=bias_total[:], in_=columns[:, ROW_BIAS:N_ROWS], axis=mybir.AxisListType.X)
+
+            w_grouped = keep.tile([P, P, PACK], BF16, name="w_grouped", align_bytes=64)
+            nc.vector.tensor_copy(out=w_grouped[:], in_=w_planes[:].rearrange("p t c -> p c t"))
+            w_codes = keep.tile([P, P], U32, name="w_codes", align_bytes=64)
+            w_scales = keep.tile([P, P], U8, name="w_scales", align_bytes=64)
+            nc.vector.quantize_mx(
+                out=w_codes[:].bitcast(FP8X4), scales=w_scales[:], in_=w_grouped[:].rearrange("p c t -> p (c t)"))
+
+            nc.vector.scalar_tensor_tensor(
+                out=feat[:, 0, :], in0=small["mc"][:], scalar=columns[:, ROW_PBM : ROW_PBM + 1], in1=spread_b[:, 1, :],
+                op0=ALU.mult, op1=ALU.mult)
+            nc.vector.scalar_tensor_tensor(
+                out=feat[:, 4, :], in0=small["mc"][:], scalar=columns[:, ROW_BBM : ROW_BBM + 1], in1=spread_b[:, 2, :],
+                op0=ALU.mult, op1=ALU.mult)
+            for m, name in ((1, "ux"), (2, "uy"), (3, "uz")):
+                nc.vector.tensor_tensor(out=feat[:, m, :], in0=small[name][:], in1=feat[:, 4, :], op=ALU.mult)
+
+            row_term = keep.tile([P, P], F32, name="row_term")
+            nc.vector.tensor_tensor(out=row_term[:], in0=small["aa1"][:], in1=small["esm1"][:], op=ALU.add)
+            col_term = keep.tile([P, P], F32, name="col_term")
+            nc.vector.tensor_tensor(out=col_term[:], in0=small["aa2"][:], in1=small["esm2"][:], op=ALU.add)
+            term_bank = psum_setup.tile([P, 2, P], F32, name="term_bank")
+            nc.tensor.transpose(term_bank[:, 0, :], row_term[:], ident_f[:])
+            nc.tensor.transpose(term_bank[:, 1, :], col_term[:], ident_f[:])
+            nc.vector.tensor_copy(out=row_term_t[:], in_=term_bank[:, 0, :])
+            nc.vector.tensor_scalar(
+                out=col_term_t[:], in0=term_bank[:, 1, :], scalar1=bias_total[:, 0:1], scalar2=None, op0=ALU.add)
+
+        psum_mx = stack.enter_context(tc.psum_pool(name="psum_mx", bufs=1))
+        psum_base = stack.enter_context(tc.psum_pool(name="psum_base", bufs=1))
+
+        for s in range(LAG_TRANSPOSE, N_STEPS):
+            step(s)

@@ -20,14 +20,32 @@ PAIRS = GROUP * P
 N_GROUPS = P // GROUP
 N_FEAT = 5
 X_AHEAD = 4
-VECTOR_COLUMNS = 2
-GPSIMD_PAIRS = 3 * PAIRS // 4
+VECTOR_NORMALISED = 3
 
 ROW_W = 0
 ROW_PBM = 5
 ROW_BBM = 6
 ROW_BIAS = 7
 N_ROWS = 13
+
+STACK_GROUPS = 16
+STACK_COLUMNS = STACK_GROUPS + STACK_GROUPS // 2
+N_STACKS = N_GROUPS // STACK_GROUPS
+STACK_ROWS = STACK_COLUMNS * N_FEAT
+
+
+def matmul_columns(g):
+    return 1 + g % 2
+
+
+def vector_columns(g):
+    return 2
+
+
+def place_in_stack(g, jj):
+    local = g % STACK_GROUPS
+    return local if jj == 0 else STACK_GROUPS + local // 2
+
 
 LAG_NORMALISE = 2
 LAG_TRANSPOSE = 3
@@ -56,7 +74,7 @@ def tile_templatepairembeddermultimer_pa_kernel(
         stack.enter_context(tc.manual_schedule())
         keep = stack.enter_context(tc.tile_pool(name="keep", bufs=1))
         x_pool = stack.enter_context(tc.tile_pool(name="x", bufs=X_AHEAD + LAG_NORMALISE + 1))
-        act_pool = stack.enter_context(tc.tile_pool(name="act", bufs=LAG_TURN_BACK + 2))
+        act_pool = stack.enter_context(tc.tile_pool(name="act", bufs=LAG_STORE + 2))
         stat_pool = stack.enter_context(tc.tile_pool(name="stat", bufs=4))
         work = stack.enter_context(tc.tile_pool(name="work", bufs=3))
         scrap = stack.enter_context(tc.tile_pool(name="scrap", bufs=4))
@@ -79,8 +97,8 @@ def tile_templatepairembeddermultimer_pa_kernel(
             nc.sync.dma_start(out=act_tiles[g][:], in_=act_dgram[:, columns_of(g), :])
 
         def vector_statistics(g):
-            vector_stats[g] = stat_pool.tile([P, VECTOR_COLUMNS, 2], F32, name="mean_var")
-            for jj in range(VECTOR_COLUMNS):
+            vector_stats[g] = stat_pool.tile([P, GROUP, 2], F32, name="mean_var")
+            for jj in range(vector_columns(g)):
                 partial = stat_pool.tile([P, 6], F32, name="partial")
                 nc.vector.bn_stats(out=partial[:], in_=x_tiles[g][:, jj, :])
                 nc.vector.bn_aggr(out=vector_stats[g][:, jj, :], in_=partial[:])
@@ -88,28 +106,30 @@ def tile_templatepairembeddermultimer_pa_kernel(
         def scalar_statistics(g):
             neg_means[g] = stat_pool.tile([P, GROUP], F32, name="neg_mean")
             stds[g] = stat_pool.tile([P, GROUP], F32, name="std")
-            row_sum = stat_pool.tile([P, GROUP - VECTOR_COLUMNS], F32, name="row_sum")
-            dev_sq = stat_pool.tile([P, GROUP - VECTOR_COLUMNS], F32, name="dev_sq")
-            for jj in range(VECTOR_COLUMNS, GROUP):
+            first = vector_columns(g)
+            row_sum = stat_pool.tile([P, GROUP], F32, name="row_sum")
+            dev_sq = stat_pool.tile([P, GROUP], F32, name="dev_sq")
+            for jj in range(first, GROUP):
                 unread = scrap.tile([P, C_IN], BF16, name="unread")
                 nc.scalar.activation(
                     out=unread[:], in_=x_tiles[g][:, jj, :], func=ACT.Identity,
-                    accum_out=row_sum[:, jj - VECTOR_COLUMNS : jj - VECTOR_COLUMNS + 1])
-            nc.scalar.mul(out=neg_means[g][:, VECTOR_COLUMNS:], in_=row_sum[:], mul=-1.0 / C_IN)
+                    accum_out=row_sum[:, jj : jj + 1])
+            nc.scalar.mul(out=neg_means[g][:, first:], in_=row_sum[:, first:], mul=-1.0 / C_IN)
             if g > 0:
                 finish_vector_statistics(g - 1)
-            for jj in range(VECTOR_COLUMNS, GROUP):
+            for jj in range(first, GROUP):
                 unread = scrap.tile([P, C_IN], BF16, name="unread")
                 nc.scalar.activation(
                     out=unread[:], in_=x_tiles[g][:, jj, :], func=ACT.Square, bias=neg_means[g][:, jj : jj + 1],
-                    scale=1.0, accum_out=dev_sq[:, jj - VECTOR_COLUMNS : jj - VECTOR_COLUMNS + 1])
+                    scale=1.0, accum_out=dev_sq[:, jj : jj + 1])
             nc.scalar.activation(
-                out=stds[g][:, VECTOR_COLUMNS:], in_=dev_sq[:], func=ACT.Sqrt, bias=eps[:, 0:1], scale=1.0 / C_IN)
+                out=stds[g][:, first:], in_=dev_sq[:, first:], func=ACT.Sqrt, bias=eps[:, 0:1], scale=1.0 / C_IN)
 
         def finish_vector_statistics(g):
-            nc.scalar.mul(out=neg_means[g][:, 0:VECTOR_COLUMNS], in_=vector_stats[g][:, :, 0], mul=-1.0)
+            n = vector_columns(g)
+            nc.scalar.mul(out=neg_means[g][:, 0:n], in_=vector_stats[g][:, 0:n, 0], mul=-1.0)
             nc.scalar.activation(
-                out=stds[g][:, 0:VECTOR_COLUMNS], in_=vector_stats[g][:, :, 1], func=ACT.Sqrt, bias=eps[:, 0:1], scale=1.0)
+                out=stds[g][:, 0:n], in_=vector_stats[g][:, 0:n, 1], func=ACT.Sqrt, bias=eps[:, 0:1], scale=1.0)
 
         def inverse_std(g):
             rstds[g] = stat_pool.tile([P, GROUP], F32, name="rstd")
@@ -118,7 +138,8 @@ def tile_templatepairembeddermultimer_pa_kernel(
         def normalise(g):
             y_tiles[g] = work.tile([P, GROUP, C_IN], F32, name="y_g")
             for jj in range(GROUP):
-                nc.gpsimd.tensor_scalar(
+                engine = nc.vector if jj < VECTOR_NORMALISED else nc.gpsimd
+                engine.tensor_scalar(
                     out=y_tiles[g][:, jj, :], in0=x_tiles[g][:, jj, :],
                     scalar1=neg_means[g][:, jj : jj + 1], scalar2=rstds[g][:, jj : jj + 1], op0=ALU.add, op1=ALU.mult)
 
@@ -142,11 +163,8 @@ def tile_templatepairembeddermultimer_pa_kernel(
             q_grouped = work.tile([P, PAIRS, PACK], BF16, name="q_grouped", align_bytes=64)
             grouped_tiles[g] = q_grouped
             nc.gpsimd.tensor_scalar(
-                out=q_grouped[:, 0:GPSIMD_PAIRS, :], in0=q_planes[:, :, 0:GPSIMD_PAIRS].rearrange("p t r -> p r t"),
+                out=q_grouped[:], in0=q_planes[:].rearrange("p t r -> p r t"),
                 scalar1=1.0, scalar2=0.0, op0=ALU.mult, op1=ALU.add)
-            nc.scalar.copy(
-                out=q_grouped[:, GPSIMD_PAIRS:, :].rearrange("p (c i) t -> p c t i", i=4),
-                in_=q_planes[:, :, GPSIMD_PAIRS:].rearrange("p t (c i) -> p c t i", i=4))
 
         def quantise(g):
             q_codes = work.tile([P, PAIRS], U32, name="q_codes", align_bytes=64)
@@ -173,8 +191,12 @@ def tile_templatepairembeddermultimer_pa_kernel(
             bases[g] = base
             for jj in range(GROUP):
                 j = g * GROUP + jj
+                by_matmul = jj < matmul_columns(g)
+                if by_matmul:
+                    nc.tensor.matmul(out=base[:, jj, :], lhsT=feat_stacks[:, g // STACK_GROUPS, :],
+                                     rhs=w_blocks[:, place_in_stack(g, jj), :], start=True, stop=False)
                 nc.tensor.matmul(out=base[:, jj, :], lhsT=col_term_t[:], rhs=ident_f[:], is_transpose=True,
-                                 start=True, stop=False)
+                                 start=not by_matmul, stop=False)
                 nc.tensor.matmul(out=base[:, jj, :], lhsT=row_term_t[:, j : j + 1].to_broadcast([P, P]), rhs=ident_f[:],
                                  is_transpose=True, start=False, stop=False)
                 nc.tensor.matmul(out=base[:, jj, :], lhsT=proj_tiles[g][:, jj, :], rhs=ident_f[:], is_transpose=True,
@@ -183,14 +205,18 @@ def tile_templatepairembeddermultimer_pa_kernel(
         def rank_one(g):
             res_tiles[g] = work.tile([P, GROUP, P], F32, name="res")
             for m in range(N_FEAT):
-                for jj in range(GROUP):
+                for jj in range(matmul_columns(g), GROUP):
                     j = g * GROUP + jj
                     nc.vector.scalar_tensor_tensor(
                         out=res_tiles[g][:, jj, :], in0=w_spread[m], scalar=feat[:, m, j : j + 1],
                         in1=act_tiles[g][:, jj, :] if m == 0 else res_tiles[g][:, jj, :], op0=ALU.mult, op1=ALU.add)
 
         def add_store(g):
-            nc.vector.tensor_tensor(out=res_tiles[g][:], in0=res_tiles[g][:], in1=bases[g][:], op=ALU.add)
+            n = matmul_columns(g)
+            nc.vector.tensor_tensor(
+                out=res_tiles[g][:, 0:n, :], in0=act_tiles[g][:, 0:n, :], in1=bases[g][:, 0:n, :], op=ALU.add)
+            nc.vector.tensor_tensor(
+                out=res_tiles[g][:, n:, :], in0=res_tiles[g][:, n:, :], in1=bases[g][:, n:, :], op=ALU.add)
             nc.sync.dma_start(out=out[:, columns_of(g), :], in_=res_tiles[g][:])
 
         def in_range(g):
@@ -203,12 +229,13 @@ def tile_templatepairembeddermultimer_pa_kernel(
                 load_act(s)
             if in_range(s - LAG_PROJECT):
                 quantise(s - LAG_PROJECT)
+            if in_range(s - LAG_NORMALISE):
+                inverse_std(s - LAG_NORMALISE)
             if in_range(s - LAG_STORE):
                 add_store(s - LAG_STORE)
             if in_range(s - LAG_REGROUP):
                 regroup(s - LAG_REGROUP)
             if in_range(s - LAG_NORMALISE):
-                inverse_std(s - LAG_NORMALISE)
                 normalise(s - LAG_NORMALISE)
             if in_range(s - LAG_TRANSPOSE):
                 transpose(s - LAG_TRANSPOSE)
@@ -261,20 +288,22 @@ def tile_templatepairembeddermultimer_pa_kernel(
             small[name] = keep.tile([P, P], BF16, name="in_" + name)
             nc.sync.dma_start(out=small[name][:], in_=matrix)
 
-        for s in range(LAG_TRANSPOSE):
+        for s in range(LAG_TRANSPOSE - 1):
             step(s)
-
         gain = keep.tile([P, PACK], F32, name="gain")
         nc.vector.tensor_copy(out=gain[:], in_=gain_in[:])
         shift = keep.tile([P, PACK], F32, name="shift")
         nc.vector.tensor_copy(out=shift[:], in_=shift_in[:])
+        for s in range(LAG_TRANSPOSE - 1, LAG_REGROUP):
+            step(s)
+
         columns = keep.tile([P, N_ROWS], F32, name="columns")
         bias_total = keep.tile([P, 1], F32, name="bias_total")
         row_term_t = keep.tile([P, P], F32, name="row_term_t")
         col_term_t = keep.tile([P, P], F32, name="col_term_t")
         feat = keep.tile([P, N_FEAT, P], F32, name="feat")
         spread_a = psum_keep.tile([P, 4, P], F32, name="spread_a")
-        spread_b = psum_keep.tile([P, 3, P], F32, name="spread_b")
+        spread_b = psum_keep.tile([P, 4, P], F32, name="spread_b")
 
         def spread(dst, row):
             nc.tensor.transpose(dst, columns[:, row : row + 1].to_broadcast([P, P]), ident_f[:])
@@ -307,19 +336,52 @@ def tile_templatepairembeddermultimer_pa_kernel(
             for m, name in ((1, "ux"), (2, "uy"), (3, "uz")):
                 nc.vector.tensor_tensor(out=feat[:, m, :], in0=small[name][:], in1=feat[:, 4, :], op=ALU.mult)
 
+            for s in range(LAG_REGROUP, LAG_PROJECT):
+                step(s)
+
             row_term = keep.tile([P, P], F32, name="row_term")
             nc.vector.tensor_tensor(out=row_term[:], in0=small["aa1"][:], in1=small["esm1"][:], op=ALU.add)
             col_term = keep.tile([P, P], F32, name="col_term")
             nc.vector.tensor_tensor(out=col_term[:], in0=small["aa2"][:], in1=small["esm2"][:], op=ALU.add)
-            term_bank = psum_setup.tile([P, 2, P], F32, name="term_bank")
+            term_bank = psum_setup.tile([P, 2 + N_STACKS, P], F32, name="term_bank")
             nc.tensor.transpose(term_bank[:, 0, :], row_term[:], ident_f[:])
             nc.tensor.transpose(term_bank[:, 1, :], col_term[:], ident_f[:])
             nc.vector.tensor_copy(out=row_term_t[:], in_=term_bank[:, 0, :])
             nc.vector.tensor_scalar(
                 out=col_term_t[:], in0=term_bank[:, 1, :], scalar1=bias_total[:, 0:1], scalar2=None, op0=ALU.add)
 
+            w_stack_t = keep.tile([P, P], F32, name="w_stack_t")
+            nc.vector.memset(w_stack_t[:], 0.0)
+            nc.vector.tensor_copy(
+                out=w_stack_t[:, 0:STACK_ROWS].rearrange("p (l m) -> p l m", m=N_FEAT),
+                in_=columns[:, ROW_W : ROW_W + N_FEAT].unsqueeze(1).to_broadcast([P, STACK_COLUMNS, N_FEAT]))
+            same_column = keep.tile([P, STACK_COLUMNS], F32, name="same_column")
+            nc.vector.reduce_sum(
+                out=same_column[:], in_=ident_f[:, 0:STACK_ROWS].rearrange("p (l m) -> p l m", m=N_FEAT),
+                axis=mybir.AxisListType.X)
+            nc.tensor.transpose(spread_b[:, 3, :], w_stack_t[:], ident_f[:])
+            w_blocks = keep.tile([P, STACK_COLUMNS, P], F32, name="w_blocks")
+            nc.vector.tensor_tensor(
+                out=w_blocks[:], in0=spread_b[:, 3, :].unsqueeze(1).to_broadcast([P, STACK_COLUMNS, P]),
+                in1=same_column[:].unsqueeze(2).to_broadcast([P, STACK_COLUMNS, P]), op=ALU.mult)
+
+            feat_cols = keep.tile([P, N_STACKS, P], F32, name="feat_cols")
+            nc.vector.memset(feat_cols[:], 0.0)
+            feat_stacks = keep.tile([P, N_STACKS, P], F32, name="feat_stacks")
+            for n in range(N_STACKS):
+                j0 = n * STACK_GROUPS * GROUP
+                j1 = j0 + STACK_GROUPS * GROUP
+                split = STACK_GROUPS * N_FEAT
+                nc.vector.tensor_copy(
+                    out=feat_cols[:, n, 0:split].rearrange("p (l m) -> p m l", m=N_FEAT), in_=feat[:, :, j0:j1:GROUP])
+                nc.vector.tensor_copy(
+                    out=feat_cols[:, n, split:STACK_ROWS].rearrange("p (l m) -> p m l", m=N_FEAT),
+                    in_=feat[:, :, j0 + GROUP + 1 : j1 : 2 * GROUP])
+                nc.tensor.transpose(term_bank[:, 2 + n, :], feat_cols[:, n, :], ident_f[:])
+            nc.vector.tensor_copy(out=feat_stacks[:], in_=term_bank[:, 2:, :])
+
         psum_mx = stack.enter_context(tc.psum_pool(name="psum_mx", bufs=1))
         psum_base = stack.enter_context(tc.psum_pool(name="psum_base", bufs=1))
 
-        for s in range(LAG_TRANSPOSE, N_STEPS):
+        for s in range(LAG_PROJECT, N_STEPS):
             step(s)

@@ -15,11 +15,13 @@ P = 128
 C_IN = 512
 PACK = 4
 LN_EPS = 1e-5
+ROOT = C_IN**-0.5
 GROUP = 4
 PAIRS = GROUP * P
 N_GROUPS = P // GROUP
 N_FEAT = 5
 X_AHEAD = 4
+VECTOR_COLUMNS = 2
 VECTOR_NORMALISED = 3
 
 ROW_W = 0
@@ -36,10 +38,6 @@ STACK_ROWS = STACK_COLUMNS * N_FEAT
 
 def matmul_columns(g):
     return 1 + g % 2
-
-
-def vector_columns(g):
-    return 2
 
 
 def place_in_stack(g, jj):
@@ -81,9 +79,8 @@ def tile_templatepairembeddermultimer_pa_kernel(
         psum_keep = stack.enter_context(tc.psum_pool(name="psum_keep", bufs=1))
         psum_y = stack.enter_context(tc.psum_pool(name="psum_y", bufs=PACK))
 
-        x_tiles, act_tiles, vector_stats, neg_means, stds, rstds, y_tiles, y_banks, plane_tiles = (
-            {}, {}, {}, {}, {}, {}, {}, {}, {})
-        grouped_tiles, code_tiles, proj_banks, proj_tiles, res_tiles, bases = {}, {}, {}, {}, {}, {}
+        x_tiles, act_tiles, stats, minus_scaled, rstds, y_tiles, y_banks, plane_tiles = {}, {}, {}, {}, {}, {}, {}, {}
+        partials, grouped_tiles, code_tiles, proj_banks, proj_tiles, res_tiles, bases = {}, {}, {}, {}, {}, {}, {}
 
         def columns_of(g):
             return slice(g * GROUP, (g + 1) * GROUP)
@@ -96,52 +93,44 @@ def tile_templatepairembeddermultimer_pa_kernel(
             act_tiles[g] = act_pool.tile([P, GROUP, P], BF16, name="act_g")
             nc.sync.dma_start(out=act_tiles[g][:], in_=act_dgram[:, columns_of(g), :])
 
-        def vector_statistics(g):
-            vector_stats[g] = stat_pool.tile([P, GROUP, 2], F32, name="mean_var")
-            for jj in range(vector_columns(g)):
-                partial = stat_pool.tile([P, 6], F32, name="partial")
-                nc.vector.bn_stats(out=partial[:], in_=x_tiles[g][:, jj, :])
-                nc.vector.bn_aggr(out=vector_stats[g][:, jj, :], in_=partial[:])
+        def bn_stats(g, jj):
+            if jj == 0:
+                stats[g] = stat_pool.tile([P, GROUP, 2], F32, name="stats")
+                partials[g] = stat_pool.tile([P, VECTOR_COLUMNS, 6], F32, name="partials")
+            nc.vector.bn_stats(out=partials[g][:, jj, :], in_=x_tiles[g][:, jj, :])
 
-        def scalar_statistics(g):
-            neg_means[g] = stat_pool.tile([P, GROUP], F32, name="neg_mean")
-            stds[g] = stat_pool.tile([P, GROUP], F32, name="std")
-            first = vector_columns(g)
-            row_sum = stat_pool.tile([P, GROUP], F32, name="row_sum")
-            dev_sq = stat_pool.tile([P, GROUP], F32, name="dev_sq")
-            for jj in range(first, GROUP):
-                unread = scrap.tile([P, C_IN], BF16, name="unread")
-                nc.scalar.activation(
-                    out=unread[:], in_=x_tiles[g][:, jj, :], func=ACT.Identity,
-                    accum_out=row_sum[:, jj : jj + 1])
-            nc.scalar.mul(out=neg_means[g][:, first:], in_=row_sum[:, first:], mul=-1.0 / C_IN)
-            if g > 0:
-                finish_vector_statistics(g - 1)
-            for jj in range(first, GROUP):
-                unread = scrap.tile([P, C_IN], BF16, name="unread")
-                nc.scalar.activation(
-                    out=unread[:], in_=x_tiles[g][:, jj, :], func=ACT.Square, bias=neg_means[g][:, jj : jj + 1],
-                    scale=1.0, accum_out=dev_sq[:, jj : jj + 1])
-            nc.scalar.activation(
-                out=stds[g][:, first:], in_=dev_sq[:, first:], func=ACT.Sqrt, bias=eps[:, 0:1], scale=1.0 / C_IN)
+        def bn_aggr(g, jj):
+            nc.vector.bn_aggr(out=stats[g][:, jj, :], in_=partials[g][:, jj, :])
 
-        def finish_vector_statistics(g):
-            n = vector_columns(g)
-            nc.scalar.mul(out=neg_means[g][:, 0:n], in_=vector_stats[g][:, 0:n, 0], mul=-1.0)
+        def row_mean(g, jj):
+            unread = scrap.tile([P, C_IN], BF16, name="unread")
             nc.scalar.activation(
-                out=stds[g][:, 0:n], in_=vector_stats[g][:, 0:n, 1], func=ACT.Sqrt, bias=eps[:, 0:1], scale=1.0)
+                out=unread[:], in_=x_tiles[g][:, jj, :], func=ACT.Identity, scale=-1.0 / C_IN,
+                accum_out=stats[g][:, jj, 0:1])
+
+        def scale_means(g):
+            minus_scaled[g] = stat_pool.tile([P, GROUP - VECTOR_COLUMNS], F32, name="minus_scaled")
+            nc.scalar.mul(out=minus_scaled[g][:], in_=stats[g][:, VECTOR_COLUMNS:, 0], mul=ROOT)
+
+        def row_variance(g, jj):
+            unread = scrap.tile([P, C_IN], BF16, name="unread")
+            n = jj - VECTOR_COLUMNS
+            nc.scalar.activation(
+                out=unread[:], in_=x_tiles[g][:, jj, :], func=ACT.Square, bias=minus_scaled[g][:, n : n + 1], scale=ROOT,
+                accum_out=stats[g][:, jj, 1:2])
 
         def inverse_std(g):
             rstds[g] = stat_pool.tile([P, GROUP], F32, name="rstd")
-            nc.vector.reciprocal(out=rstds[g][:], in_=stds[g][:])
+            nc.scalar.activation(
+                out=rstds[g][:], in_=stats[g][:, :, 1], func=ACT.Abs_reciprocal_sqrt, bias=eps[:, 0:1], scale=1.0)
 
-        def normalise(g):
-            y_tiles[g] = work.tile([P, GROUP, C_IN], F32, name="y_g")
-            for jj in range(GROUP):
-                engine = nc.vector if jj < VECTOR_NORMALISED else nc.gpsimd
-                engine.tensor_scalar(
-                    out=y_tiles[g][:, jj, :], in0=x_tiles[g][:, jj, :],
-                    scalar1=neg_means[g][:, jj : jj + 1], scalar2=rstds[g][:, jj : jj + 1], op0=ALU.add, op1=ALU.mult)
+        def normalise(g, jj):
+            if jj == 0:
+                y_tiles[g] = work.tile([P, GROUP, C_IN], F32, name="y_g")
+            engine = nc.vector if jj < VECTOR_NORMALISED else nc.gpsimd
+            engine.tensor_scalar(
+                out=y_tiles[g][:, jj, :], in0=x_tiles[g][:, jj, :], scalar1=stats[g][:, jj, 0:1],
+                scalar2=rstds[g][:, jj : jj + 1], op0=ALU.subtract if jj < VECTOR_COLUMNS else ALU.add, op1=ALU.mult)
 
         def transpose(g):
             y_banks[g] = []
@@ -151,12 +140,12 @@ def tile_templatepairembeddermultimer_pa_kernel(
                     nc.tensor.transpose(y_t[:, jj, :], y_tiles[g][:, jj, t:C_IN:PACK], ident_f[:])
                 y_banks[g].append(y_t)
 
-        def gain_shift(g):
-            plane_tiles[g] = work.tile([P, PACK, PAIRS], BF16, name="q_planes")
-            for t in range(PACK):
-                nc.scalar.activation(
-                    out=plane_tiles[g][:, t, :], in_=y_banks[g][t][:].rearrange("p a b -> p (a b)"), func=ACT.Identity,
-                    scale=gain[:, t : t + 1], bias=shift[:, t : t + 1])
+        def gain_shift(g, t):
+            if t == 0:
+                plane_tiles[g] = work.tile([P, PACK, PAIRS], BF16, name="q_planes")
+            nc.scalar.activation(
+                out=plane_tiles[g][:, t, :], in_=y_banks[g][t][:].rearrange("p a b -> p (a b)"), func=ACT.Identity,
+                scale=gain[:, t : t + 1], bias=shift[:, t : t + 1])
 
         def regroup(g):
             q_planes = plane_tiles[g]
@@ -202,19 +191,22 @@ def tile_templatepairembeddermultimer_pa_kernel(
                 nc.tensor.matmul(out=base[:, jj, :], lhsT=proj_tiles[g][:, jj, :], rhs=ident_f[:], is_transpose=True,
                                  start=False, stop=True)
 
-        def rank_one(g):
-            res_tiles[g] = work.tile([P, GROUP, P], F32, name="res")
-            for m in range(N_FEAT):
-                for jj in range(matmul_columns(g), GROUP):
-                    j = g * GROUP + jj
-                    nc.vector.scalar_tensor_tensor(
-                        out=res_tiles[g][:, jj, :], in0=w_spread[m], scalar=feat[:, m, j : j + 1],
-                        in1=act_tiles[g][:, jj, :] if m == 0 else res_tiles[g][:, jj, :], op0=ALU.mult, op1=ALU.add)
+        def rank_one(g, m):
+            if m == 0:
+                res_tiles[g] = work.tile([P, GROUP, P], F32, name="res")
+            for jj in range(matmul_columns(g), GROUP):
+                j = g * GROUP + jj
+                nc.vector.scalar_tensor_tensor(
+                    out=res_tiles[g][:, jj, :], in0=w_spread[m], scalar=feat[:, m, j : j + 1],
+                    in1=act_tiles[g][:, jj, :] if m == 0 else res_tiles[g][:, jj, :], op0=ALU.mult, op1=ALU.add)
 
-        def add_store(g):
+        def add_matmul_columns(g):
             n = matmul_columns(g)
             nc.vector.tensor_tensor(
                 out=res_tiles[g][:, 0:n, :], in0=act_tiles[g][:, 0:n, :], in1=bases[g][:, 0:n, :], op=ALU.add)
+
+        def add_others_store(g):
+            n = matmul_columns(g)
             nc.vector.tensor_tensor(
                 out=res_tiles[g][:, n:, :], in0=res_tiles[g][:, n:, :], in1=bases[g][:, n:, :], op=ALU.add)
             nc.sync.dma_start(out=out[:, columns_of(g), :], in_=res_tiles[g][:])
@@ -223,44 +215,32 @@ def tile_templatepairembeddermultimer_pa_kernel(
             return 0 <= g < N_GROUPS
 
         def step(s):
-            if in_range(s + X_AHEAD):
-                load_x(s + X_AHEAD)
-            if in_range(s):
-                load_act(s)
-            if in_range(s - LAG_PROJECT):
-                quantise(s - LAG_PROJECT)
-            if in_range(s - LAG_NORMALISE):
-                inverse_std(s - LAG_NORMALISE)
-            if in_range(s - LAG_STORE):
-                add_store(s - LAG_STORE)
-            if in_range(s - LAG_REGROUP):
-                regroup(s - LAG_REGROUP)
-            if in_range(s - LAG_NORMALISE):
-                normalise(s - LAG_NORMALISE)
-            if in_range(s - LAG_TRANSPOSE):
-                transpose(s - LAG_TRANSPOSE)
-            if in_range(s - LAG_PROJECT):
-                project(s - LAG_PROJECT)
-            if in_range(s - LAG_TURN_BACK):
-                turn_back(s - LAG_TURN_BACK)
-            if in_range(s):
-                vector_statistics(s)
-                scalar_statistics(s)
-            if s == N_GROUPS:
-                finish_vector_statistics(N_GROUPS - 1)
-            if in_range(s - LAG_TRANSPOSE):
-                gain_shift(s - LAG_TRANSPOSE)
-            if in_range(s - LAG_PROJECT):
-                copy_out(s - LAG_PROJECT)
-            if in_range(s - LAG_TURN_BACK):
-                rank_one(s - LAG_TURN_BACK)
+            def run(calls):
+                for call, g, *rest in calls:
+                    if in_range(g):
+                        call(g, *rest)
+
+            normalised, turned, regrouped = s - LAG_NORMALISE, s - LAG_TRANSPOSE, s - LAG_REGROUP
+            projected, back, stored = s - LAG_PROJECT, s - LAG_TURN_BACK, s - LAG_STORE
+            run([(load_x, s + X_AHEAD), (load_act, s)])
+            run([
+                (quantise, projected), (bn_stats, s, 0), (rank_one, back, 0), (add_matmul_columns, stored),
+                (rank_one, back, 1), (add_others_store, stored), (rank_one, back, 2), (normalise, normalised, 0),
+                (bn_aggr, s, 0), (bn_stats, s, 1), (rank_one, back, 3), (normalise, normalised, 1),
+                (normalise, normalised, 2), (rank_one, back, 4), (bn_aggr, s, 1)])
+            run([(regroup, regrouped), (normalise, normalised, 3)])
+            run([(transpose, turned), (project, projected), (turn_back, back)])
+            run([
+                (inverse_std, s - 1), (row_mean, s, 2), (row_mean, s, 3), (gain_shift, turned, 0), (scale_means, s),
+                (gain_shift, turned, 1), (row_variance, s, 2), (row_variance, s, 3), (gain_shift, turned, 2),
+                (gain_shift, turned, 3), (copy_out, projected)])
 
         eps = keep.tile([P, 1], F32, name="eps")
         nc.vector.memset(eps[:], LN_EPS)
         rows = keep.tile([P, P], BF16, name="rows")
         nc.vector.memset(rows[:], 0.0)
         table_warm = keep.tile([P, 1], F32, name="table_warm")
-        nc.scalar.activation(out=table_warm[:], in_=eps[:], func=ACT.Sqrt)
+        nc.scalar.activation(out=table_warm[:], in_=eps[:], func=ACT.Abs_reciprocal_sqrt)
         ident_f = keep.tile([P, P], F32, name="ident_f")
         make_identity(nc, ident_f[:])
         ident_b = keep.tile([P, P], BF16, name="ident_b")

@@ -22,7 +22,6 @@ N_GROUPS = P // GROUP
 N_FEAT = 5
 X_AHEAD = 4
 VECTOR_COLUMNS = 2
-VECTOR_NORMALISED = 3
 
 ROW_W = 0
 ROW_PBM = 5
@@ -80,7 +79,7 @@ def tile_templatepairembeddermultimer_pa_kernel(
         psum_y = stack.enter_context(tc.psum_pool(name="psum_y", bufs=PACK))
 
         x_tiles, act_tiles, stats, minus_scaled, rstds, y_tiles, y_banks, plane_tiles = {}, {}, {}, {}, {}, {}, {}, {}
-        partials, grouped_tiles, code_tiles, proj_banks, proj_tiles, res_tiles, bases = {}, {}, {}, {}, {}, {}, {}
+        gates, partials, grouped_tiles, code_tiles, proj_banks, proj_tiles, res_tiles, bases = {}, {}, {}, {}, {}, {}, {}, {}
 
         def columns_of(g):
             return slice(g * GROUP, (g + 1) * GROUP)
@@ -127,8 +126,7 @@ def tile_templatepairembeddermultimer_pa_kernel(
         def normalise(g, jj):
             if jj == 0:
                 y_tiles[g] = work.tile([P, GROUP, C_IN], F32, name="y_g")
-            engine = nc.vector if jj < VECTOR_NORMALISED else nc.gpsimd
-            engine.tensor_scalar(
+            nc.vector.tensor_scalar(
                 out=y_tiles[g][:, jj, :], in0=x_tiles[g][:, jj, :], scalar1=stats[g][:, jj, 0:1],
                 scalar2=rstds[g][:, jj : jj + 1], op0=ALU.subtract if jj < VECTOR_COLUMNS else ALU.add, op1=ALU.mult)
 
@@ -147,13 +145,17 @@ def tile_templatepairembeddermultimer_pa_kernel(
                 out=plane_tiles[g][:, t, :], in_=y_banks[g][t][:].rearrange("p a b -> p (a b)"), func=ACT.Identity,
                 scale=gain[:, t : t + 1], bias=shift[:, t : t + 1])
 
+        def open_gate(g):
+            gates[g] = stat_pool.tile([P, 1], F32, name="gate")
+            nc.vector.memset(gates[g][:], 1.0)
+
         def regroup(g):
             q_planes = plane_tiles[g]
             q_grouped = work.tile([P, PAIRS, PACK], BF16, name="q_grouped", align_bytes=64)
             grouped_tiles[g] = q_grouped
             nc.gpsimd.tensor_scalar(
                 out=q_grouped[:], in0=q_planes[:].rearrange("p t r -> p r t"),
-                scalar1=1.0, scalar2=0.0, op0=ALU.mult, op1=ALU.add)
+                scalar1=gates[g][:, 0:1], scalar2=0.0, op0=ALU.mult, op1=ALU.add)
 
         def quantise(g):
             q_codes = work.tile([P, PAIRS], U32, name="q_codes", align_bytes=64)
@@ -223,12 +225,11 @@ def tile_templatepairembeddermultimer_pa_kernel(
             normalised, turned, regrouped = s - LAG_NORMALISE, s - LAG_TRANSPOSE, s - LAG_REGROUP
             projected, back, stored = s - LAG_PROJECT, s - LAG_TURN_BACK, s - LAG_STORE
             run([(load_x, s + X_AHEAD), (load_act, s)])
-            run([
-                (quantise, projected), (bn_stats, s, 0), (rank_one, back, 0), (add_matmul_columns, stored),
-                (rank_one, back, 1), (add_others_store, stored), (rank_one, back, 2), (normalise, normalised, 0),
-                (bn_aggr, s, 0), (bn_stats, s, 1), (rank_one, back, 3), (normalise, normalised, 1),
-                (normalise, normalised, 2), (rank_one, back, 4), (bn_aggr, s, 1)])
-            run([(regroup, regrouped), (normalise, normalised, 3)])
+            run([(quantise, projected)] + [(normalise, normalised, jj) for jj in range(GROUP)] + [
+                (open_gate, regrouped), (bn_stats, s, 0), (rank_one, back, 0), (add_matmul_columns, stored),
+                (rank_one, back, 1), (add_others_store, stored), (rank_one, back, 2),
+                (bn_aggr, s, 0), (bn_stats, s, 1), (rank_one, back, 3), (rank_one, back, 4), (bn_aggr, s, 1)])
+            run([(regroup, regrouped)])
             run([(transpose, turned), (project, projected), (turn_back, back)])
             run([
                 (inverse_std, s - 1), (row_mean, s, 2), (row_mean, s, 3), (gain_shift, turned, 0), (scale_means, s),

@@ -15,6 +15,7 @@ P = 128
 C_IN = 512
 PACK = 4
 LN_EPS = 1e-5
+VECTOR_NORMALISED = 3
 ROOT = C_IN**-0.5
 GROUP = 4
 PAIRS = GROUP * P
@@ -126,7 +127,8 @@ def tile_templatepairembeddermultimer_pa_kernel(
         def normalise(g, jj):
             if jj == 0:
                 y_tiles[g] = work.tile([P, GROUP, C_IN], F32, name="y_g")
-            nc.vector.tensor_scalar(
+            engine = nc.vector if jj < VECTOR_NORMALISED else nc.gpsimd
+            engine.tensor_scalar(
                 out=y_tiles[g][:, jj, :], in0=x_tiles[g][:, jj, :], scalar1=stats[g][:, jj, 0:1],
                 scalar2=rstds[g][:, jj : jj + 1], op0=ALU.subtract if jj < VECTOR_COLUMNS else ALU.add, op1=ALU.mult)
 
@@ -225,11 +227,12 @@ def tile_templatepairembeddermultimer_pa_kernel(
             normalised, turned, regrouped = s - LAG_NORMALISE, s - LAG_TRANSPOSE, s - LAG_REGROUP
             projected, back, stored = s - LAG_PROJECT, s - LAG_TURN_BACK, s - LAG_STORE
             run([(load_x, s + X_AHEAD), (load_act, s)])
-            run([(quantise, projected)] + [(normalise, normalised, jj) for jj in range(GROUP)] + [
-                (open_gate, regrouped), (bn_stats, s, 0), (rank_one, back, 0), (add_matmul_columns, stored),
-                (rank_one, back, 1), (add_others_store, stored), (rank_one, back, 2),
-                (bn_aggr, s, 0), (bn_stats, s, 1), (rank_one, back, 3), (rank_one, back, 4), (bn_aggr, s, 1)])
+            run([(quantise, projected)] + [(normalise, normalised, jj) for jj in range(VECTOR_NORMALISED)] + [
+                (open_gate, regrouped), (add_matmul_columns, stored), (add_others_store, stored), (rank_one, back, 0),
+                (bn_stats, s, 0), (rank_one, back, 1), (bn_stats, s, 1), (rank_one, back, 2), (bn_aggr, s, 0),
+                (rank_one, back, 3), (bn_aggr, s, 1), (rank_one, back, 4)])
             run([(regroup, regrouped)])
+            run([(normalise, normalised, jj) for jj in range(VECTOR_NORMALISED, GROUP)])
             run([(transpose, turned), (project, projected), (turn_back, back)])
             run([
                 (inverse_std, s - 1), (row_mean, s, 2), (row_mean, s, 3), (gain_shift, turned, 0), (scale_means, s),

@@ -126,10 +126,10 @@ def tile_templatepairembeddermultimer_pa_kernel(
 
         def normalise(g, jj):
             if jj == 0:
-                y_tiles[g] = work.tile([P, GROUP, C_IN], F32, name="y_g")
+                y_tiles[g] = work.tile([P, GROUP, PACK, P], F32, name="y_g")
             engine = nc.vector if jj < VECTOR_NORMALISED else nc.gpsimd
             engine.tensor_scalar(
-                out=y_tiles[g][:, jj, :], in0=x_tiles[g][:, jj, :], scalar1=stats[g][:, jj, 0:1],
+                out=y_tiles[g][:, jj, :, :], in0=x_tiles[g][:, jj, :].rearrange("i (p t) -> i t p", t=PACK), scalar1=stats[g][:, jj, 0:1],
                 scalar2=rstds[g][:, jj : jj + 1], op0=ALU.subtract if jj < VECTOR_COLUMNS else ALU.add, op1=ALU.mult)
 
         def transpose(g):
@@ -137,7 +137,7 @@ def tile_templatepairembeddermultimer_pa_kernel(
             for t in range(PACK):
                 y_t = psum_y.tile([P, GROUP, P], F32, name="y_t")
                 for jj in range(GROUP):
-                    nc.tensor.transpose(y_t[:, jj, :], y_tiles[g][:, jj, t:C_IN:PACK], ident_f[:])
+                    nc.tensor.transpose(y_t[:, jj, :], y_tiles[g][:, jj, t, :], ident_f[:])
                 y_banks[g].append(y_t)
 
         def gain_shift(g, t):

@@ -15,14 +15,11 @@ P = 128
 C_IN = 512
 PACK = 4
 LN_EPS = 1e-5
-VECTOR_NORMALISED = 3
-ROOT = C_IN**-0.5
 GROUP = 4
 PAIRS = GROUP * P
 N_GROUPS = P // GROUP
 N_FEAT = 5
 X_AHEAD = 4
-VECTOR_COLUMNS = 2
 
 ROW_W = 0
 ROW_PBM = 5
@@ -40,6 +37,10 @@ def matmul_columns(g):
     return 1 + g % 2
 
 
+def vector_normalised(g):
+    return GROUP - g % 2
+
+
 def place_in_stack(g, jj):
     local = g % STACK_GROUPS
     return local if jj == 0 else STACK_GROUPS + local // 2
@@ -52,6 +53,7 @@ LAG_PROJECT = 5
 LAG_TURN_BACK = 6
 LAG_STORE = 7
 N_STEPS = N_GROUPS + LAG_STORE
+FIRST_LATE_GROUP = N_GROUPS - LAG_REGROUP + LAG_NORMALISE - 1
 
 FLOPS = 2 * P * P * C_IN * P
 
@@ -75,12 +77,11 @@ def tile_templatepairembeddermultimer_pa_kernel(
         act_pool = stack.enter_context(tc.tile_pool(name="act", bufs=LAG_STORE + 2))
         stat_pool = stack.enter_context(tc.tile_pool(name="stat", bufs=4))
         work = stack.enter_context(tc.tile_pool(name="work", bufs=3))
-        scrap = stack.enter_context(tc.tile_pool(name="scrap", bufs=4))
-        psum_keep = stack.enter_context(tc.psum_pool(name="psum_keep", bufs=1))
         psum_y = stack.enter_context(tc.psum_pool(name="psum_y", bufs=PACK))
 
-        x_tiles, act_tiles, stats, minus_scaled, rstds, y_tiles, y_banks, plane_tiles = {}, {}, {}, {}, {}, {}, {}, {}
-        gates, partials, grouped_tiles, code_tiles, proj_banks, proj_tiles, res_tiles, bases = {}, {}, {}, {}, {}, {}, {}, {}
+        x_tiles, act_tiles, stats, minus_means, rstds, y_tiles, y_banks, plane_tiles = {}, {}, {}, {}, {}, {}, {}, {}
+        product_tiles, term_banks, term_tiles = {}, {}, {}
+        partials, grouped_tiles, code_tiles, proj_banks, proj_tiles, bases = {}, {}, {}, {}, {}, {}
 
         def columns_of(g):
             return slice(g * GROUP, (g + 1) * GROUP)
@@ -96,41 +97,32 @@ def tile_templatepairembeddermultimer_pa_kernel(
         def bn_stats(g, jj):
             if jj == 0:
                 stats[g] = stat_pool.tile([P, GROUP, 2], F32, name="stats")
-                partials[g] = stat_pool.tile([P, VECTOR_COLUMNS, 6], F32, name="partials")
+                partials[g] = stat_pool.tile([P, GROUP, 6], F32, name="partials")
             nc.vector.bn_stats(out=partials[g][:, jj, :], in_=x_tiles[g][:, jj, :])
 
         def bn_aggr(g, jj):
             nc.vector.bn_aggr(out=stats[g][:, jj, :], in_=partials[g][:, jj, :])
 
-        def row_mean(g, jj):
-            unread = scrap.tile([P, C_IN], BF16, name="unread")
-            nc.scalar.activation(
-                out=unread[:], in_=x_tiles[g][:, jj, :], func=ACT.Identity, scale=-1.0 / C_IN,
-                accum_out=stats[g][:, jj, 0:1])
-
-        def scale_means(g):
-            minus_scaled[g] = stat_pool.tile([P, GROUP - VECTOR_COLUMNS], F32, name="minus_scaled")
-            nc.scalar.mul(out=minus_scaled[g][:], in_=stats[g][:, VECTOR_COLUMNS:, 0], mul=ROOT)
-
-        def row_variance(g, jj):
-            unread = scrap.tile([P, C_IN], BF16, name="unread")
-            n = jj - VECTOR_COLUMNS
-            nc.scalar.activation(
-                out=unread[:], in_=x_tiles[g][:, jj, :], func=ACT.Square, bias=minus_scaled[g][:, n : n + 1], scale=ROOT,
-                accum_out=stats[g][:, jj, 1:2])
-
         def inverse_std(g):
             rstds[g] = stat_pool.tile([P, GROUP], F32, name="rstd")
             nc.scalar.activation(
                 out=rstds[g][:], in_=stats[g][:, :, 1], func=ACT.Abs_reciprocal_sqrt, bias=eps[:, 0:1], scale=1.0)
+            if vector_normalised(g) < GROUP:
+                minus_means[g] = stat_pool.tile([P, 1], F32, name="minus_mean")
+                nc.scalar.mul(out=minus_means[g][:], in_=stats[g][:, GROUP - 1, 0:1], mul=-1.0)
 
         def normalise(g, jj):
             if jj == 0:
                 y_tiles[g] = work.tile([P, GROUP, PACK, P], F32, name="y_g")
-            engine = nc.vector if jj < VECTOR_NORMALISED else nc.gpsimd
-            engine.tensor_scalar(
-                out=y_tiles[g][:, jj, :, :], in0=x_tiles[g][:, jj, :].rearrange("i (p t) -> i t p", t=PACK), scalar1=stats[g][:, jj, 0:1],
-                scalar2=rstds[g][:, jj : jj + 1], op0=ALU.subtract if jj < VECTOR_COLUMNS else ALU.add, op1=ALU.mult)
+            out = y_tiles[g][:, jj, :, :]
+            x = x_tiles[g][:, jj, :].rearrange("i (p t) -> i t p", t=PACK)
+            rstd = rstds[g][:, jj : jj + 1]
+            if jj < vector_normalised(g):
+                nc.vector.tensor_scalar(
+                    out=out, in0=x, scalar1=stats[g][:, jj, 0:1], scalar2=rstd, op0=ALU.subtract, op1=ALU.mult)
+            else:
+                nc.gpsimd.tensor_scalar(
+                    out=out, in0=x, scalar1=minus_means[g][:, 0:1], scalar2=rstd, op0=ALU.add, op1=ALU.mult)
 
         def transpose(g):
             y_banks[g] = []
@@ -147,17 +139,16 @@ def tile_templatepairembeddermultimer_pa_kernel(
                 out=plane_tiles[g][:, t, :], in_=y_banks[g][t][:].rearrange("p a b -> p (a b)"), func=ACT.Identity,
                 scale=gain[:, t : t + 1], bias=shift[:, t : t + 1])
 
-        def open_gate(g):
-            gates[g] = stat_pool.tile([P, 1], F32, name="gate")
-            nc.vector.memset(gates[g][:], 1.0)
-
         def regroup(g):
-            q_planes = plane_tiles[g]
-            q_grouped = work.tile([P, PAIRS, PACK], BF16, name="q_grouped", align_bytes=64)
-            grouped_tiles[g] = q_grouped
-            nc.gpsimd.tensor_scalar(
-                out=q_grouped[:], in0=q_planes[:].rearrange("p t r -> p r t"),
-                scalar1=gates[g][:, 0:1], scalar2=0.0, op0=ALU.mult, op1=ALU.add)
+            grouped_tiles[g] = work.tile([P, PAIRS, PACK], BF16, name="q_grouped", align_bytes=64)
+            planes = plane_tiles[g][:].rearrange("p t r -> p r t")
+            if g < FIRST_LATE_GROUP:
+                gate = stat_pool.tile([P, 1], F32, name="gate")
+                nc.vector.memset(gate[:], 1.0)
+                nc.gpsimd.tensor_scalar(
+                    out=grouped_tiles[g][:], in0=planes, scalar1=gate[:, 0:1], scalar2=0.0, op0=ALU.mult, op1=ALU.add)
+            else:
+                nc.vector.tensor_copy(out=grouped_tiles[g][:], in_=planes)
 
         def quantise(g):
             q_codes = work.tile([P, PAIRS], U32, name="q_codes", align_bytes=64)
@@ -179,6 +170,33 @@ def tile_templatepairembeddermultimer_pa_kernel(
             proj_tiles[g] = work.tile([P, GROUP, P], F32, name="proj_t")
             nc.scalar.copy(out=proj_tiles[g][:].rearrange("p a b -> p (a b)"), in_=proj_banks[g][:])
 
+        def other_columns(g):
+            return range(matmul_columns(g), GROUP)
+
+        def products(g, jj):
+            if jj == matmul_columns(g):
+                product_tiles[g] = work.tile([P, GROUP, N_FEAT, P], F32, name="products")
+            j = g * GROUP + jj
+            for m in range(N_FEAT):
+                nc.scalar.activation(
+                    out=product_tiles[g][:, jj, m, :], in_=w_spread[:, m, :], func=ACT.Copy, scale=feat[:, m, j : j + 1])
+
+        def add_up(g):
+            term_banks[g] = psum_terms.tile([P, GROUP, P], F32, name="term_ps")
+            for jj in other_columns(g):
+                for m in range(N_FEAT):
+                    nc.tensor.matmul(
+                        out=term_banks[g][:, jj, :], lhsT=product_tiles[g][:, jj, m, :], rhs=ident_f[:],
+                        is_transpose=True, start=m == 0, stop=m == N_FEAT - 1)
+
+        def copy_terms(g):
+            term_tiles[g] = work.tile([P, GROUP, P], F32, name="term_t")
+            for jj in other_columns(g):
+                j = g * GROUP + jj
+                nc.scalar.activation(
+                    out=term_tiles[g][:, jj, :], in_=term_banks[g][:, jj, :], func=ACT.Identity,
+                    bias=row_term_t[:, j : j + 1], scale=1.0)
+
         def turn_back(g):
             base = psum_base.tile([P, GROUP, P], F32, name="base")
             bases[g] = base
@@ -190,30 +208,15 @@ def tile_templatepairembeddermultimer_pa_kernel(
                                      rhs=w_blocks[:, place_in_stack(g, jj), :], start=True, stop=False)
                 nc.tensor.matmul(out=base[:, jj, :], lhsT=col_term_t[:], rhs=ident_f[:], is_transpose=True,
                                  start=not by_matmul, stop=False)
-                nc.tensor.matmul(out=base[:, jj, :], lhsT=row_term_t[:, j : j + 1].to_broadcast([P, P]), rhs=ident_f[:],
-                                 is_transpose=True, start=False, stop=False)
+                terms = row_term_t[:, j : j + 1].to_broadcast([P, P]) if by_matmul else term_tiles[g][:, jj, :]
+                nc.tensor.matmul(out=base[:, jj, :], lhsT=terms, rhs=ident_f[:], is_transpose=True, start=False, stop=False)
                 nc.tensor.matmul(out=base[:, jj, :], lhsT=proj_tiles[g][:, jj, :], rhs=ident_f[:], is_transpose=True,
                                  start=False, stop=True)
 
-        def rank_one(g, m):
-            if m == 0:
-                res_tiles[g] = work.tile([P, GROUP, P], F32, name="res")
-            for jj in range(matmul_columns(g), GROUP):
-                j = g * GROUP + jj
-                nc.vector.scalar_tensor_tensor(
-                    out=res_tiles[g][:, jj, :], in0=w_spread[m], scalar=feat[:, m, j : j + 1],
-                    in1=act_tiles[g][:, jj, :] if m == 0 else res_tiles[g][:, jj, :], op0=ALU.mult, op1=ALU.add)
-
-        def add_matmul_columns(g):
-            n = matmul_columns(g)
-            nc.vector.tensor_tensor(
-                out=res_tiles[g][:, 0:n, :], in0=act_tiles[g][:, 0:n, :], in1=bases[g][:, 0:n, :], op=ALU.add)
-
-        def add_others_store(g):
-            n = matmul_columns(g)
-            nc.vector.tensor_tensor(
-                out=res_tiles[g][:, n:, :], in0=res_tiles[g][:, n:, :], in1=bases[g][:, n:, :], op=ALU.add)
-            nc.sync.dma_start(out=out[:, columns_of(g), :], in_=res_tiles[g][:])
+        def add_store(g):
+            res = work.tile([P, GROUP, P], F32, name="res")
+            nc.vector.tensor_tensor(out=res[:], in0=act_tiles[g][:], in1=bases[g][:], op=ALU.add)
+            nc.sync.dma_start(out=out[:, columns_of(g), :], in_=res[:])
 
         def in_range(g):
             return 0 <= g < N_GROUPS
@@ -227,17 +230,20 @@ def tile_templatepairembeddermultimer_pa_kernel(
             normalised, turned, regrouped = s - LAG_NORMALISE, s - LAG_TRANSPOSE, s - LAG_REGROUP
             projected, back, stored = s - LAG_PROJECT, s - LAG_TURN_BACK, s - LAG_STORE
             run([(load_x, s + X_AHEAD), (load_act, s)])
-            run([(quantise, projected)] + [(normalise, normalised, jj) for jj in range(VECTOR_NORMALISED)] + [
-                (open_gate, regrouped), (add_matmul_columns, stored), (add_others_store, stored), (rank_one, back, 0),
-                (bn_stats, s, 0), (rank_one, back, 1), (bn_stats, s, 1), (rank_one, back, 2), (bn_aggr, s, 0),
-                (rank_one, back, 3), (bn_aggr, s, 1), (rank_one, back, 4)])
-            run([(regroup, regrouped)])
-            run([(normalise, normalised, jj) for jj in range(VECTOR_NORMALISED, GROUP)])
-            run([(transpose, turned), (project, projected), (turn_back, back)])
-            run([
-                (inverse_std, s - 1), (row_mean, s, 2), (row_mean, s, 3), (gain_shift, turned, 0), (scale_means, s),
-                (gain_shift, turned, 1), (row_variance, s, 2), (row_variance, s, 3), (gain_shift, turned, 2),
-                (gain_shift, turned, 3), (copy_out, projected)])
+            run([(quantise, projected)])
+            if in_range(normalised):
+                run([(normalise, normalised, jj) for jj in range(vector_normalised(normalised))])
+            run([(regroup, regrouped), (add_store, stored)])
+            run([(bn_stats, s, jj) for jj in range(GROUP)] + [(bn_aggr, s, jj) for jj in range(GROUP)])
+            if in_range(normalised):
+                run([(normalise, normalised, jj) for jj in range(vector_normalised(normalised), GROUP)])
+            run([(transpose, turned), (add_up, projected), (project, projected), (turn_back, back)])
+            run([(inverse_std, s - 1)])
+            for t in range(PACK):
+                if in_range(regrouped) and t in other_columns(regrouped):
+                    products(regrouped, t)
+                run([(gain_shift, turned, t)])
+            run([(copy_terms, projected), (copy_out, projected)])
 
         eps = keep.tile([P, 1], F32, name="eps")
         nc.vector.memset(eps[:], LN_EPS)
@@ -275,37 +281,38 @@ def tile_templatepairembeddermultimer_pa_kernel(
         for s in range(LAG_TRANSPOSE - 1):
             step(s)
         gain = keep.tile([P, PACK], F32, name="gain")
-        nc.vector.tensor_copy(out=gain[:], in_=gain_in[:])
+        nc.scalar.copy(out=gain[:], in_=gain_in[:])
         shift = keep.tile([P, PACK], F32, name="shift")
-        nc.vector.tensor_copy(out=shift[:], in_=shift_in[:])
-        for s in range(LAG_TRANSPOSE - 1, LAG_REGROUP):
-            step(s)
+        nc.scalar.copy(out=shift[:], in_=shift_in[:])
+        step(LAG_TRANSPOSE - 1)
 
         columns = keep.tile([P, N_ROWS], F32, name="columns")
         bias_total = keep.tile([P, 1], F32, name="bias_total")
         row_term_t = keep.tile([P, P], F32, name="row_term_t")
         col_term_t = keep.tile([P, P], F32, name="col_term_t")
         feat = keep.tile([P, N_FEAT, P], F32, name="feat")
-        spread_a = psum_keep.tile([P, 4, P], F32, name="spread_a")
-        spread_b = psum_keep.tile([P, 4, P], F32, name="spread_b")
+        w_spread = keep.tile([P, N_FEAT, P], F32, name="w_spread")
 
         def spread(dst, row):
             nc.tensor.transpose(dst, columns[:, row : row + 1].to_broadcast([P, P]), ident_f[:])
 
         with tc.psum_pool(name="psum_setup", bufs=1) as psum_setup:
+            spread_a = psum_setup.tile([P, 4, P], F32, name="spread_a")
+            spread_b = psum_setup.tile([P, 4, P], F32, name="spread_b")
             rows_t = psum_setup.tile([P, P], BF16, name="rows_t")
             nc.tensor.transpose(rows_t[:], rows[:], ident_b[:])
-            nc.vector.tensor_copy(out=columns[:], in_=rows_t[:, 0:N_ROWS])
+            nc.scalar.copy(out=columns[:], in_=rows_t[:, 0:N_ROWS])
             for m in range(4):
                 spread(spread_a[:, m, :], ROW_W + m)
             spread(spread_b[:, 0, :], ROW_W + 4)
             spread(spread_b[:, 1, :], ROW_PBM)
             spread(spread_b[:, 2, :], ROW_BBM)
-            w_spread = [spread_a[:, m, :] for m in range(4)] + [spread_b[:, 0, :]]
+            nc.scalar.copy(out=w_spread[:, 0:4, :], in_=spread_a[:])
+            nc.scalar.copy(out=w_spread[:, 4, :], in_=spread_b[:, 0, :])
             nc.vector.reduce_sum(out=bias_total[:], in_=columns[:, ROW_BIAS:N_ROWS], axis=mybir.AxisListType.X)
 
             w_grouped = keep.tile([P, P, PACK], BF16, name="w_grouped", align_bytes=64)
-            nc.vector.tensor_copy(out=w_grouped[:], in_=w_planes[:].rearrange("p t c -> p c t"))
+            nc.scalar.copy(out=w_grouped[:], in_=w_planes[:].rearrange("p t c -> p c t"))
             w_codes = keep.tile([P, P], U32, name="w_codes", align_bytes=64)
             w_scales = keep.tile([P, P], U8, name="w_scales", align_bytes=64)
             nc.vector.quantize_mx(
@@ -320,23 +327,22 @@ def tile_templatepairembeddermultimer_pa_kernel(
             for m, name in ((1, "ux"), (2, "uy"), (3, "uz")):
                 nc.vector.tensor_tensor(out=feat[:, m, :], in0=small[name][:], in1=feat[:, 4, :], op=ALU.mult)
 
-            for s in range(LAG_REGROUP, LAG_PROJECT):
-                step(s)
+            step(LAG_TRANSPOSE)
 
             row_term = keep.tile([P, P], F32, name="row_term")
-            nc.vector.tensor_tensor(out=row_term[:], in0=small["aa1"][:], in1=small["esm1"][:], op=ALU.add)
+            nc.gpsimd.tensor_tensor(out=row_term[:], in0=small["aa1"][:], in1=small["esm1"][:], op=ALU.add)
             col_term = keep.tile([P, P], F32, name="col_term")
-            nc.vector.tensor_tensor(out=col_term[:], in0=small["aa2"][:], in1=small["esm2"][:], op=ALU.add)
+            nc.gpsimd.tensor_tensor(out=col_term[:], in0=small["aa2"][:], in1=small["esm2"][:], op=ALU.add)
             term_bank = psum_setup.tile([P, 2 + N_STACKS, P], F32, name="term_bank")
             nc.tensor.transpose(term_bank[:, 0, :], row_term[:], ident_f[:])
             nc.tensor.transpose(term_bank[:, 1, :], col_term[:], ident_f[:])
-            nc.vector.tensor_copy(out=row_term_t[:], in_=term_bank[:, 0, :])
-            nc.vector.tensor_scalar(
-                out=col_term_t[:], in0=term_bank[:, 1, :], scalar1=bias_total[:, 0:1], scalar2=None, op0=ALU.add)
+            nc.scalar.copy(out=row_term_t[:], in_=term_bank[:, 0, :])
+            nc.scalar.activation(
+                out=col_term_t[:], in_=term_bank[:, 1, :], func=ACT.Identity, bias=bias_total[:, 0:1], scale=1.0)
 
             w_stack_t = keep.tile([P, P], F32, name="w_stack_t")
-            nc.vector.memset(w_stack_t[:], 0.0)
-            nc.vector.tensor_copy(
+            nc.gpsimd.memset(w_stack_t[:], 0.0)
+            nc.scalar.copy(
                 out=w_stack_t[:, 0:STACK_ROWS].rearrange("p (l m) -> p l m", m=N_FEAT),
                 in_=columns[:, ROW_W : ROW_W + N_FEAT].unsqueeze(1).to_broadcast([P, STACK_COLUMNS, N_FEAT]))
             same_column = keep.tile([P, STACK_COLUMNS], F32, name="same_column")
@@ -345,27 +351,29 @@ def tile_templatepairembeddermultimer_pa_kernel(
                 axis=mybir.AxisListType.X)
             nc.tensor.transpose(spread_b[:, 3, :], w_stack_t[:], ident_f[:])
             w_blocks = keep.tile([P, STACK_COLUMNS, P], F32, name="w_blocks")
-            nc.vector.tensor_tensor(
-                out=w_blocks[:], in0=spread_b[:, 3, :].unsqueeze(1).to_broadcast([P, STACK_COLUMNS, P]),
-                in1=same_column[:].unsqueeze(2).to_broadcast([P, STACK_COLUMNS, P]), op=ALU.mult)
+            for l in range(STACK_COLUMNS):
+                nc.scalar.activation(
+                    out=w_blocks[:, l, :], in_=spread_b[:, 3, :], func=ACT.Copy, scale=same_column[:, l : l + 1])
 
             feat_cols = keep.tile([P, N_STACKS, P], F32, name="feat_cols")
-            nc.vector.memset(feat_cols[:], 0.0)
+            nc.gpsimd.memset(feat_cols[:], 0.0)
             feat_stacks = keep.tile([P, N_STACKS, P], F32, name="feat_stacks")
             for n in range(N_STACKS):
                 j0 = n * STACK_GROUPS * GROUP
                 j1 = j0 + STACK_GROUPS * GROUP
                 split = STACK_GROUPS * N_FEAT
-                nc.vector.tensor_copy(
+                nc.scalar.copy(
                     out=feat_cols[:, n, 0:split].rearrange("p (l m) -> p m l", m=N_FEAT), in_=feat[:, :, j0:j1:GROUP])
-                nc.vector.tensor_copy(
+                nc.scalar.copy(
                     out=feat_cols[:, n, split:STACK_ROWS].rearrange("p (l m) -> p m l", m=N_FEAT),
                     in_=feat[:, :, j0 + GROUP + 1 : j1 : 2 * GROUP])
                 nc.tensor.transpose(term_bank[:, 2 + n, :], feat_cols[:, n, :], ident_f[:])
-            nc.vector.tensor_copy(out=feat_stacks[:], in_=term_bank[:, 2:, :])
+            nc.scalar.copy(out=feat_stacks[:], in_=term_bank[:, 2:, :])
+            step(LAG_REGROUP)
 
         psum_mx = stack.enter_context(tc.psum_pool(name="psum_mx", bufs=1))
-        psum_base = stack.enter_context(tc.psum_pool(name="psum_base", bufs=1))
+        psum_terms = stack.enter_context(tc.psum_pool(name="psum_terms", bufs=1))
+        psum_base = stack.enter_context(tc.psum_pool(name="psum_base", bufs=2))
 
         for s in range(LAG_PROJECT, N_STEPS):
             step(s)

@@ -29,31 +29,37 @@ N_ROWS = 13
 
 STACK_GROUPS = 16
 STACK_COLUMNS = STACK_GROUPS + STACK_GROUPS // 2
-N_STACKS = N_GROUPS // STACK_GROUPS
+FULL_STACKS = N_GROUPS // STACK_GROUPS
+N_STACKS = FULL_STACKS + 1
 STACK_ROWS = STACK_COLUMNS * N_FEAT
+EXTRA_EVERY = 8
+EXTRA_GROUPS = range(EXTRA_EVERY, N_GROUPS, EXTRA_EVERY)
 
 
 def matmul_columns(g):
-    return 1 + g % 2
+    return 2 if g % 2 == 1 or g in EXTRA_GROUPS else 1
 
 
 def vector_normalised(g):
-    return GROUP - g % 2
+    return GROUP - 1
 
 
 def place_in_stack(g, jj):
-    local = g % STACK_GROUPS
-    return local if jj == 0 else STACK_GROUPS + local // 2
+    tile, local = divmod(g, STACK_GROUPS)
+    if jj == 0:
+        return tile, local
+    if g % 2 == 1:
+        return tile, STACK_GROUPS + local // 2
+    return FULL_STACKS, EXTRA_GROUPS.index(g)
 
 
-LAG_NORMALISE = 2
-LAG_TRANSPOSE = 3
-LAG_REGROUP = 4
-LAG_PROJECT = 5
-LAG_TURN_BACK = 6
-LAG_STORE = 7
-N_STEPS = N_GROUPS + LAG_STORE
-FIRST_LATE_GROUP = N_GROUPS - LAG_REGROUP + LAG_NORMALISE - 1
+LAG_NORMALISE = 1
+LAG_TRANSPOSE = 2
+LAG_REGROUP = 3
+LAG_PROJECT = 4
+LAG_TURN_BACK = 5
+N_STEPS = N_GROUPS + LAG_TURN_BACK
+FIRST_LATE_GROUP = N_GROUPS - LAG_REGROUP
 
 FLOPS = 2 * P * P * C_IN * P
 
@@ -74,7 +80,7 @@ def tile_templatepairembeddermultimer_pa_kernel(
         stack.enter_context(tc.manual_schedule())
         keep = stack.enter_context(tc.tile_pool(name="keep", bufs=1))
         x_pool = stack.enter_context(tc.tile_pool(name="x", bufs=X_AHEAD + LAG_NORMALISE + 1))
-        act_pool = stack.enter_context(tc.tile_pool(name="act", bufs=LAG_STORE + 2))
+        act_pool = stack.enter_context(tc.tile_pool(name="act", bufs=LAG_TURN_BACK + 2))
         stat_pool = stack.enter_context(tc.tile_pool(name="stat", bufs=4))
         work = stack.enter_context(tc.tile_pool(name="work", bufs=3))
         psum_y = stack.enter_context(tc.psum_pool(name="psum_y", bufs=PACK))
@@ -168,7 +174,8 @@ def tile_templatepairembeddermultimer_pa_kernel(
 
         def copy_out(g):
             proj_tiles[g] = work.tile([P, GROUP, P], F32, name="proj_t")
-            nc.scalar.copy(out=proj_tiles[g][:].rearrange("p a b -> p (a b)"), in_=proj_banks[g][:])
+            copy = nc.vector.tensor_copy if g % 4 == 3 else nc.scalar.copy
+            copy(out=proj_tiles[g][:].rearrange("p a b -> p (a b)"), in_=proj_banks[g][:])
 
         def other_columns(g):
             return range(matmul_columns(g), GROUP)
@@ -191,11 +198,8 @@ def tile_templatepairembeddermultimer_pa_kernel(
 
         def copy_terms(g):
             term_tiles[g] = work.tile([P, GROUP, P], F32, name="term_t")
-            for jj in other_columns(g):
-                j = g * GROUP + jj
-                nc.scalar.activation(
-                    out=term_tiles[g][:, jj, :], in_=term_banks[g][:, jj, :], func=ACT.Identity,
-                    bias=row_term_t[:, j : j + 1], scale=1.0)
+            n = matmul_columns(g)
+            nc.scalar.copy(out=term_tiles[g][:, n:, :], in_=term_banks[g][:, n:, :])
 
         def turn_back(g):
             base = psum_base.tile([P, GROUP, P], F32, name="base")
@@ -204,12 +208,16 @@ def tile_templatepairembeddermultimer_pa_kernel(
                 j = g * GROUP + jj
                 by_matmul = jj < matmul_columns(g)
                 if by_matmul:
-                    nc.tensor.matmul(out=base[:, jj, :], lhsT=feat_stacks[:, g // STACK_GROUPS, :],
-                                     rhs=w_blocks[:, place_in_stack(g, jj), :], start=True, stop=False)
+                    tile, local = place_in_stack(g, jj)
+                    nc.tensor.matmul(out=base[:, jj, :], lhsT=feat_stacks[:, tile, :], rhs=w_blocks[:, local, :],
+                                     start=True, stop=False)
                 nc.tensor.matmul(out=base[:, jj, :], lhsT=col_term_t[:], rhs=ident_f[:], is_transpose=True,
                                  start=not by_matmul, stop=False)
-                terms = row_term_t[:, j : j + 1].to_broadcast([P, P]) if by_matmul else term_tiles[g][:, jj, :]
-                nc.tensor.matmul(out=base[:, jj, :], lhsT=terms, rhs=ident_f[:], is_transpose=True, start=False, stop=False)
+                nc.tensor.matmul(out=base[:, jj, :], lhsT=row_term_t[:, j : j + 1].to_broadcast([P, P]), rhs=ident_f[:],
+                                 is_transpose=True, start=False, stop=False)
+                if not by_matmul:
+                    nc.tensor.matmul(out=base[:, jj, :], lhsT=term_tiles[g][:, jj, :], rhs=ident_f[:], is_transpose=True,
+                                     start=False, stop=False)
                 nc.tensor.matmul(out=base[:, jj, :], lhsT=proj_tiles[g][:, jj, :], rhs=ident_f[:], is_transpose=True,
                                  start=False, stop=True)
 
@@ -228,22 +236,29 @@ def tile_templatepairembeddermultimer_pa_kernel(
                         call(g, *rest)
 
             normalised, turned, regrouped = s - LAG_NORMALISE, s - LAG_TRANSPOSE, s - LAG_REGROUP
-            projected, back, stored = s - LAG_PROJECT, s - LAG_TURN_BACK, s - LAG_STORE
+            projected, back = s - LAG_PROJECT, s - LAG_TURN_BACK
             run([(load_x, s + X_AHEAD), (load_act, s)])
-            run([(quantise, projected)])
-            if in_range(normalised):
-                run([(normalise, normalised, jj) for jj in range(vector_normalised(normalised))])
-            run([(regroup, regrouped), (add_store, stored)])
-            run([(bn_stats, s, jj) for jj in range(GROUP)] + [(bn_aggr, s, jj) for jj in range(GROUP)])
-            if in_range(normalised):
-                run([(normalise, normalised, jj) for jj in range(vector_normalised(normalised), GROUP)])
-            run([(transpose, turned), (add_up, projected), (project, projected), (turn_back, back)])
-            run([(inverse_std, s - 1)])
+            run([(transpose, turned), (add_up, projected), (turn_back, back)])
+            if s > LAG_TRANSPOSE:
+                run([(inverse_std, normalised)])
             for t in range(PACK):
                 if in_range(regrouped) and t in other_columns(regrouped):
                     products(regrouped, t)
                 run([(gain_shift, turned, t)])
-            run([(copy_terms, projected), (copy_out, projected)])
+            if s <= LAG_TRANSPOSE:
+                run([(inverse_std, normalised)])
+            run([(copy_terms, projected)])
+            statistics = [(bn_stats, s, jj) for jj in range(GROUP)] + [(bn_aggr, s, jj) for jj in range(GROUP)]
+            normalisation = []
+            if in_range(normalised):
+                normalisation = [(normalise, normalised, jj) for jj in range(GROUP)]
+            if s < LAG_TRANSPOSE:
+                run(normalisation + statistics)
+            else:
+                run(statistics + [(quantise, projected)] + normalisation)
+            run([(regroup, regrouped), (add_store, back)])
+            run([(project, projected)])
+            run([(copy_out, projected)])
 
         eps = keep.tile([P, 1], F32, name="eps")
         nc.vector.memset(eps[:], LN_EPS)
@@ -255,6 +270,14 @@ def tile_templatepairembeddermultimer_pa_kernel(
         make_identity(nc, ident_f[:])
         ident_b = keep.tile([P, P], BF16, name="ident_b")
         make_identity(nc, ident_b[:])
+        same_column = keep.tile([P, STACK_COLUMNS], F32, name="same_column")
+        nc.vector.reduce_sum(
+            out=same_column[:], in_=ident_f[:, 0:STACK_ROWS].rearrange("p (l m) -> p l m", m=N_FEAT),
+            axis=mybir.AxisListType.X)
+        w_stack_t = keep.tile([P, P], F32, name="w_stack_t")
+        nc.gpsimd.memset(w_stack_t[:], 0.0)
+        feat_cols = keep.tile([P, N_STACKS, P], F32, name="feat_cols")
+        nc.gpsimd.memset(feat_cols[:], 0.0)
 
         load_x(0)
         load_x(1)
@@ -278,13 +301,12 @@ def tile_templatepairembeddermultimer_pa_kernel(
             small[name] = keep.tile([P, P], BF16, name="in_" + name)
             nc.sync.dma_start(out=small[name][:], in_=matrix)
 
-        for s in range(LAG_TRANSPOSE - 1):
+        for s in range(LAG_TRANSPOSE):
             step(s)
         gain = keep.tile([P, PACK], F32, name="gain")
         nc.scalar.copy(out=gain[:], in_=gain_in[:])
         shift = keep.tile([P, PACK], F32, name="shift")
         nc.scalar.copy(out=shift[:], in_=shift_in[:])
-        step(LAG_TRANSPOSE - 1)
 
         columns = keep.tile([P, N_ROWS], F32, name="columns")
         bias_total = keep.tile([P, 1], F32, name="bias_total")
@@ -302,6 +324,24 @@ def tile_templatepairembeddermultimer_pa_kernel(
             rows_t = psum_setup.tile([P, P], BF16, name="rows_t")
             nc.tensor.transpose(rows_t[:], rows[:], ident_b[:])
             nc.scalar.copy(out=columns[:], in_=rows_t[:, 0:N_ROWS])
+            step(LAG_TRANSPOSE)
+
+            row_term = keep.tile([P, P], F32, name="row_term")
+            nc.gpsimd.tensor_tensor(out=row_term[:], in0=small["aa1"][:], in1=small["esm1"][:], op=ALU.add)
+            col_term = keep.tile([P, P], F32, name="col_term")
+            nc.gpsimd.tensor_tensor(out=col_term[:], in0=small["aa2"][:], in1=small["esm2"][:], op=ALU.add)
+
+            nc.scalar.copy(
+                out=w_stack_t[:, 0:STACK_ROWS].rearrange("p (l m) -> p l m", m=N_FEAT),
+                in_=columns[:, ROW_W : ROW_W + N_FEAT].unsqueeze(1).to_broadcast([P, STACK_COLUMNS, N_FEAT]))
+            nc.tensor.transpose(spread_b[:, 3, :], w_stack_t[:], ident_f[:])
+            w_blocks = keep.tile([P, STACK_COLUMNS, P], F32, name="w_blocks")
+            w_stack = keep.tile([P, P], F32, name="w_stack")
+            nc.scalar.copy(out=w_stack[:], in_=spread_b[:, 3, :])
+            nc.gpsimd.tensor_tensor(
+                out=w_blocks[:], in0=w_stack[:].unsqueeze(1).to_broadcast([P, STACK_COLUMNS, P]),
+                in1=same_column[:].unsqueeze(2).to_broadcast([P, STACK_COLUMNS, P]), op=ALU.mult)
+
             for m in range(4):
                 spread(spread_a[:, m, :], ROW_W + m)
             spread(spread_b[:, 0, :], ROW_W + 4)
@@ -327,38 +367,15 @@ def tile_templatepairembeddermultimer_pa_kernel(
             for m, name in ((1, "ux"), (2, "uy"), (3, "uz")):
                 nc.vector.tensor_tensor(out=feat[:, m, :], in0=small[name][:], in1=feat[:, 4, :], op=ALU.mult)
 
-            step(LAG_TRANSPOSE)
-
-            row_term = keep.tile([P, P], F32, name="row_term")
-            nc.gpsimd.tensor_tensor(out=row_term[:], in0=small["aa1"][:], in1=small["esm1"][:], op=ALU.add)
-            col_term = keep.tile([P, P], F32, name="col_term")
-            nc.gpsimd.tensor_tensor(out=col_term[:], in0=small["aa2"][:], in1=small["esm2"][:], op=ALU.add)
-            term_bank = psum_setup.tile([P, 2 + N_STACKS, P], F32, name="term_bank")
+            term_bank = psum_setup.tile([P, 2, P], F32, name="term_bank")
             nc.tensor.transpose(term_bank[:, 0, :], row_term[:], ident_f[:])
             nc.tensor.transpose(term_bank[:, 1, :], col_term[:], ident_f[:])
             nc.scalar.copy(out=row_term_t[:], in_=term_bank[:, 0, :])
             nc.scalar.activation(
                 out=col_term_t[:], in_=term_bank[:, 1, :], func=ACT.Identity, bias=bias_total[:, 0:1], scale=1.0)
 
-            w_stack_t = keep.tile([P, P], F32, name="w_stack_t")
-            nc.gpsimd.memset(w_stack_t[:], 0.0)
-            nc.scalar.copy(
-                out=w_stack_t[:, 0:STACK_ROWS].rearrange("p (l m) -> p l m", m=N_FEAT),
-                in_=columns[:, ROW_W : ROW_W + N_FEAT].unsqueeze(1).to_broadcast([P, STACK_COLUMNS, N_FEAT]))
-            same_column = keep.tile([P, STACK_COLUMNS], F32, name="same_column")
-            nc.vector.reduce_sum(
-                out=same_column[:], in_=ident_f[:, 0:STACK_ROWS].rearrange("p (l m) -> p l m", m=N_FEAT),
-                axis=mybir.AxisListType.X)
-            nc.tensor.transpose(spread_b[:, 3, :], w_stack_t[:], ident_f[:])
-            w_blocks = keep.tile([P, STACK_COLUMNS, P], F32, name="w_blocks")
-            for l in range(STACK_COLUMNS):
-                nc.scalar.activation(
-                    out=w_blocks[:, l, :], in_=spread_b[:, 3, :], func=ACT.Copy, scale=same_column[:, l : l + 1])
-
-            feat_cols = keep.tile([P, N_STACKS, P], F32, name="feat_cols")
-            nc.gpsimd.memset(feat_cols[:], 0.0)
             feat_stacks = keep.tile([P, N_STACKS, P], F32, name="feat_stacks")
-            for n in range(N_STACKS):
+            for n in range(FULL_STACKS):
                 j0 = n * STACK_GROUPS * GROUP
                 j1 = j0 + STACK_GROUPS * GROUP
                 split = STACK_GROUPS * N_FEAT
@@ -367,13 +384,16 @@ def tile_templatepairembeddermultimer_pa_kernel(
                 nc.scalar.copy(
                     out=feat_cols[:, n, split:STACK_ROWS].rearrange("p (l m) -> p m l", m=N_FEAT),
                     in_=feat[:, :, j0 + GROUP + 1 : j1 : 2 * GROUP])
-                nc.tensor.transpose(term_bank[:, 2 + n, :], feat_cols[:, n, :], ident_f[:])
-            nc.scalar.copy(out=feat_stacks[:], in_=term_bank[:, 2:, :])
-            step(LAG_REGROUP)
+            nc.scalar.copy(
+                out=feat_cols[:, FULL_STACKS, 0 : len(EXTRA_GROUPS) * N_FEAT].rearrange("p (l m) -> p m l", m=N_FEAT),
+                in_=feat[:, :, EXTRA_EVERY * GROUP + 1 : P : EXTRA_EVERY * GROUP])
+            for n in range(N_STACKS):
+                nc.tensor.transpose(spread_a[:, n, :], feat_cols[:, n, :], ident_f[:])
+            nc.scalar.copy(out=feat_stacks[:], in_=spread_a[:, 0:N_STACKS, :])
 
         psum_mx = stack.enter_context(tc.psum_pool(name="psum_mx", bufs=1))
         psum_terms = stack.enter_context(tc.psum_pool(name="psum_terms", bufs=1))
         psum_base = stack.enter_context(tc.psum_pool(name="psum_base", bufs=2))
 
-        for s in range(LAG_PROJECT, N_STEPS):
+        for s in range(LAG_REGROUP, N_STEPS):
             step(s)

@@ -27,11 +27,11 @@ ROW_BBM = 6
 ROW_BIAS = 7
 N_ROWS = 13
 
-STACK_GROUPS = 16
-STACK_COLUMNS = STACK_GROUPS + STACK_GROUPS // 2
-FULL_STACKS = N_GROUPS // STACK_GROUPS
-N_STACKS = FULL_STACKS + 1
+STACK_COLUMNS = 8
 STACK_ROWS = STACK_COLUMNS * N_FEAT
+FIRST_STACKS = N_GROUPS // STACK_COLUMNS
+ODD_STACKS = N_GROUPS // 2 // STACK_COLUMNS
+N_STACKS = FIRST_STACKS + ODD_STACKS + 1
 EXTRA_EVERY = 8
 EXTRA_GROUPS = range(EXTRA_EVERY, N_GROUPS, EXTRA_EVERY)
 
@@ -40,17 +40,13 @@ def matmul_columns(g):
     return 2 if g % 2 == 1 or g in EXTRA_GROUPS else 1
 
 
-def vector_normalised(g):
-    return GROUP - 1
-
-
 def place_in_stack(g, jj):
-    tile, local = divmod(g, STACK_GROUPS)
     if jj == 0:
-        return tile, local
+        return divmod(g, STACK_COLUMNS)
     if g % 2 == 1:
-        return tile, STACK_GROUPS + local // 2
-    return FULL_STACKS, EXTRA_GROUPS.index(g)
+        tile, local = divmod(g // 2, STACK_COLUMNS)
+        return FIRST_STACKS + tile, local
+    return N_STACKS - 1, EXTRA_GROUPS.index(g)
 
 
 LAG_NORMALISE = 1
@@ -85,7 +81,7 @@ def tile_templatepairembeddermultimer_pa_kernel(
         work = stack.enter_context(tc.tile_pool(name="work", bufs=3))
         psum_y = stack.enter_context(tc.psum_pool(name="psum_y", bufs=PACK))
 
-        x_tiles, act_tiles, stats, minus_means, rstds, y_tiles, y_banks, plane_tiles = {}, {}, {}, {}, {}, {}, {}, {}
+        x_tiles, act_tiles, stats, rstds, y_tiles, y_banks, plane_tiles = {}, {}, {}, {}, {}, {}, {}
         product_tiles, term_banks, term_tiles = {}, {}, {}
         partials, grouped_tiles, code_tiles, proj_banks, proj_tiles, bases = {}, {}, {}, {}, {}, {}
 
@@ -113,22 +109,13 @@ def tile_templatepairembeddermultimer_pa_kernel(
             rstds[g] = stat_pool.tile([P, GROUP], F32, name="rstd")
             nc.scalar.activation(
                 out=rstds[g][:], in_=stats[g][:, :, 1], func=ACT.Abs_reciprocal_sqrt, bias=eps[:, 0:1], scale=1.0)
-            if vector_normalised(g) < GROUP:
-                minus_means[g] = stat_pool.tile([P, 1], F32, name="minus_mean")
-                nc.scalar.mul(out=minus_means[g][:], in_=stats[g][:, GROUP - 1, 0:1], mul=-1.0)
 
-        def normalise(g, jj):
-            if jj == 0:
-                y_tiles[g] = work.tile([P, GROUP, PACK, P], F32, name="y_g")
-            out = y_tiles[g][:, jj, :, :]
-            x = x_tiles[g][:, jj, :].rearrange("i (p t) -> i t p", t=PACK)
-            rstd = rstds[g][:, jj : jj + 1]
-            if jj < vector_normalised(g):
+        def normalise(g):
+            y_tiles[g] = work.tile([P, GROUP, PACK, P], F32, name="y_g")
+            for jj in range(GROUP):
                 nc.vector.tensor_scalar(
-                    out=out, in0=x, scalar1=stats[g][:, jj, 0:1], scalar2=rstd, op0=ALU.subtract, op1=ALU.mult)
-            else:
-                nc.gpsimd.tensor_scalar(
-                    out=out, in0=x, scalar1=minus_means[g][:, 0:1], scalar2=rstd, op0=ALU.add, op1=ALU.mult)
+                    out=y_tiles[g][:, jj, :, :], in0=x_tiles[g][:, jj, :].rearrange("i (p t) -> i t p", t=PACK),
+                    scalar1=stats[g][:, jj, 0:1], scalar2=rstds[g][:, jj : jj + 1], op0=ALU.subtract, op1=ALU.mult)
 
         def transpose(g):
             y_banks[g] = []
@@ -149,10 +136,9 @@ def tile_templatepairembeddermultimer_pa_kernel(
             grouped_tiles[g] = work.tile([P, PAIRS, PACK], BF16, name="q_grouped", align_bytes=64)
             planes = plane_tiles[g][:].rearrange("p t r -> p r t")
             if g < FIRST_LATE_GROUP:
-                gate = stat_pool.tile([P, 1], F32, name="gate")
-                nc.vector.memset(gate[:], 1.0)
+                nc.vector.memset(grouped_tiles[g][:, 0, 0:1], 0.0)
                 nc.gpsimd.tensor_scalar(
-                    out=grouped_tiles[g][:], in0=planes, scalar1=gate[:, 0:1], scalar2=0.0, op0=ALU.mult, op1=ALU.add)
+                    out=grouped_tiles[g][:], in0=planes, scalar1=1.0, scalar2=0.0, op0=ALU.mult, op1=ALU.add)
             else:
                 nc.vector.tensor_copy(out=grouped_tiles[g][:], in_=planes)
 
@@ -174,8 +160,7 @@ def tile_templatepairembeddermultimer_pa_kernel(
 
         def copy_out(g):
             proj_tiles[g] = work.tile([P, GROUP, P], F32, name="proj_t")
-            copy = nc.vector.tensor_copy if g % 4 == 3 else nc.scalar.copy
-            copy(out=proj_tiles[g][:].rearrange("p a b -> p (a b)"), in_=proj_banks[g][:])
+            nc.scalar.copy(out=proj_tiles[g][:].rearrange("p a b -> p (a b)"), in_=proj_banks[g][:])
 
         def other_columns(g):
             return range(matmul_columns(g), GROUP)
@@ -249,13 +234,10 @@ def tile_templatepairembeddermultimer_pa_kernel(
                 run([(inverse_std, normalised)])
             run([(copy_terms, projected)])
             statistics = [(bn_stats, s, jj) for jj in range(GROUP)] + [(bn_aggr, s, jj) for jj in range(GROUP)]
-            normalisation = []
-            if in_range(normalised):
-                normalisation = [(normalise, normalised, jj) for jj in range(GROUP)]
             if s < LAG_TRANSPOSE:
-                run(normalisation + statistics)
+                run([(normalise, normalised)] + statistics)
             else:
-                run(statistics + [(quantise, projected)] + normalisation)
+                run(statistics + [(quantise, projected), (normalise, normalised)])
             run([(regroup, regrouped), (add_store, back)])
             run([(project, projected)])
             run([(copy_out, projected)])
@@ -326,6 +308,10 @@ def tile_templatepairembeddermultimer_pa_kernel(
             nc.scalar.copy(out=columns[:], in_=rows_t[:, 0:N_ROWS])
             step(LAG_TRANSPOSE)
 
+            w_grouped = keep.tile([P, P, PACK], BF16, name="w_grouped", align_bytes=64)
+            nc.gpsimd.tensor_scalar(
+                out=w_grouped[:], in0=w_planes[:].rearrange("p t c -> p c t"),
+                scalar1=1.0, scalar2=0.0, op0=ALU.mult, op1=ALU.add)
             row_term = keep.tile([P, P], F32, name="row_term")
             nc.gpsimd.tensor_tensor(out=row_term[:], in0=small["aa1"][:], in1=small["esm1"][:], op=ALU.add)
             col_term = keep.tile([P, P], F32, name="col_term")
@@ -351,8 +337,6 @@ def tile_templatepairembeddermultimer_pa_kernel(
             nc.scalar.copy(out=w_spread[:, 4, :], in_=spread_b[:, 0, :])
             nc.vector.reduce_sum(out=bias_total[:], in_=columns[:, ROW_BIAS:N_ROWS], axis=mybir.AxisListType.X)
 
-            w_grouped = keep.tile([P, P, PACK], BF16, name="w_grouped", align_bytes=64)
-            nc.scalar.copy(out=w_grouped[:], in_=w_planes[:].rearrange("p t c -> p c t"))
             w_codes = keep.tile([P, P], U32, name="w_codes", align_bytes=64)
             w_scales = keep.tile([P, P], U8, name="w_scales", align_bytes=64)
             nc.vector.quantize_mx(
@@ -367,7 +351,7 @@ def tile_templatepairembeddermultimer_pa_kernel(
             for m, name in ((1, "ux"), (2, "uy"), (3, "uz")):
                 nc.vector.tensor_tensor(out=feat[:, m, :], in0=small[name][:], in1=feat[:, 4, :], op=ALU.mult)
 
-            term_bank = psum_setup.tile([P, 2, P], F32, name="term_bank")
+            term_bank = psum_setup.tile([P, 4, P], F32, name="term_bank")
             nc.tensor.transpose(term_bank[:, 0, :], row_term[:], ident_f[:])
             nc.tensor.transpose(term_bank[:, 1, :], col_term[:], ident_f[:])
             nc.scalar.copy(out=row_term_t[:], in_=term_bank[:, 0, :])
@@ -375,25 +359,28 @@ def tile_templatepairembeddermultimer_pa_kernel(
                 out=col_term_t[:], in_=term_bank[:, 1, :], func=ACT.Identity, bias=bias_total[:, 0:1], scale=1.0)
 
             feat_stacks = keep.tile([P, N_STACKS, P], F32, name="feat_stacks")
-            for n in range(FULL_STACKS):
-                j0 = n * STACK_GROUPS * GROUP
-                j1 = j0 + STACK_GROUPS * GROUP
-                split = STACK_GROUPS * N_FEAT
-                nc.scalar.copy(
-                    out=feat_cols[:, n, 0:split].rearrange("p (l m) -> p m l", m=N_FEAT), in_=feat[:, :, j0:j1:GROUP])
-                nc.scalar.copy(
-                    out=feat_cols[:, n, split:STACK_ROWS].rearrange("p (l m) -> p m l", m=N_FEAT),
-                    in_=feat[:, :, j0 + GROUP + 1 : j1 : 2 * GROUP])
-            nc.scalar.copy(
-                out=feat_cols[:, FULL_STACKS, 0 : len(EXTRA_GROUPS) * N_FEAT].rearrange("p (l m) -> p m l", m=N_FEAT),
-                in_=feat[:, :, EXTRA_EVERY * GROUP + 1 : P : EXTRA_EVERY * GROUP])
-            for n in range(N_STACKS):
-                nc.tensor.transpose(spread_a[:, n, :], feat_cols[:, n, :], ident_f[:])
-            nc.scalar.copy(out=feat_stacks[:], in_=spread_a[:, 0:N_STACKS, :])
+            for first, last, j0, j_step in (
+                (0, FIRST_STACKS, 0, GROUP),
+                (FIRST_STACKS, N_STACKS - 1, GROUP + 1, 2 * GROUP),
+                (N_STACKS - 1, N_STACKS, EXTRA_EVERY * GROUP + 1, EXTRA_EVERY * GROUP),
+            ):
+                for n in range(first, last):
+                    j = j0 + (n - first) * STACK_COLUMNS * j_step
+                    n_columns = len(range(j, P, j_step)[:STACK_COLUMNS])
+                    nc.gpsimd.tensor_scalar(
+                        out=feat_cols[:, n, 0 : n_columns * N_FEAT].rearrange("p (l m) -> p m l", m=N_FEAT),
+                        in0=feat[:, :, j : j + (n_columns - 1) * j_step + 1 : j_step],
+                        scalar1=1.0, scalar2=0.0, op0=ALU.mult, op1=ALU.add)
+            step(LAG_REGROUP)
+            banks = [spread_a[:, 0:4, :], term_bank[:, 2:4, :], spread_b[:, 3:4, :]]
+            for n0, bank in zip((0, 4, 6), banks):
+                for n in range(bank.shape[1]):
+                    nc.tensor.transpose(bank[:, n, :], feat_cols[:, n0 + n, :], ident_f[:])
+                nc.vector.tensor_copy(out=feat_stacks[:, n0 : n0 + bank.shape[1], :], in_=bank)
 
         psum_mx = stack.enter_context(tc.psum_pool(name="psum_mx", bufs=1))
         psum_terms = stack.enter_context(tc.psum_pool(name="psum_terms", bufs=1))
         psum_base = stack.enter_context(tc.psum_pool(name="psum_base", bufs=2))
 
-        for s in range(LAG_REGROUP, N_STEPS):
+        for s in range(LAG_PROJECT, N_STEPS):
             step(s)

@@ -19,6 +19,7 @@ GROUP = 4
 PAIRS = GROUP * P
 N_GROUPS = P // GROUP
 N_FEAT = 5
+GPSIMD_PAIRS = 7 * PAIRS // 8
 X_AHEAD = 4
 
 ROW_W = 0
@@ -38,6 +39,10 @@ EXTRA_GROUPS = range(EXTRA_EVERY, N_GROUPS, EXTRA_EVERY)
 
 def matmul_columns(g):
     return 2 if g % 2 == 1 or g in EXTRA_GROUPS else 1
+
+
+def products_step(g):
+    return g + (LAG_REGROUP if g < N_GROUPS // 2 else LAG_TRANSPOSE)
 
 
 def place_in_stack(g, jj):
@@ -136,9 +141,11 @@ def tile_templatepairembeddermultimer_pa_kernel(
             grouped_tiles[g] = work.tile([P, PAIRS, PACK], BF16, name="q_grouped", align_bytes=64)
             planes = plane_tiles[g][:].rearrange("p t r -> p r t")
             if g < FIRST_LATE_GROUP:
-                nc.vector.memset(grouped_tiles[g][:, 0, 0:1], 0.0)
+                n = GPSIMD_PAIRS
+                nc.vector.tensor_copy(out=grouped_tiles[g][:, n - PACK :, :], in_=planes[:, n - PACK :, :])
                 nc.gpsimd.tensor_scalar(
-                    out=grouped_tiles[g][:], in0=planes, scalar1=1.0, scalar2=0.0, op0=ALU.mult, op1=ALU.add)
+                    out=grouped_tiles[g][:, 0:n, :], in0=planes[:, 0:n, :],
+                    scalar1=1.0, scalar2=0.0, op0=ALU.mult, op1=ALU.add)
             else:
                 nc.vector.tensor_copy(out=grouped_tiles[g][:], in_=planes)
 
@@ -227,8 +234,9 @@ def tile_templatepairembeddermultimer_pa_kernel(
             if s > LAG_TRANSPOSE:
                 run([(inverse_std, normalised)])
             for t in range(PACK):
-                if in_range(regrouped) and t in other_columns(regrouped):
-                    products(regrouped, t)
+                for g in (regrouped, turned):
+                    if in_range(g) and s == products_step(g) and t in other_columns(g):
+                        products(g, t)
                 run([(gain_shift, turned, t)])
             if s <= LAG_TRANSPOSE:
                 run([(inverse_std, normalised)])
@@ -269,12 +277,11 @@ def tile_templatepairembeddermultimer_pa_kernel(
         nc.sync.dma_start(out=shift_in[:], in_=ln_b.rearrange("(p t) -> p t", t=PACK))
         for n, row in enumerate((w_pbm, w_x, w_y, w_z, w_bb, as_row(pseudo_beta_mask), as_row(backbone_mask))):
             nc.sync.dma_start(out=rows[ROW_W + n : ROW_W + n + 1, :], in_=row)
-        load_x(2)
         for n, vector in enumerate((b_q, b_pbm, b_x, b_y, b_z, b_bb)):
             nc.sync.dma_start(out=rows[ROW_BIAS + n : ROW_BIAS + n + 1, :], in_=as_row(vector))
+        load_x(2)
         w_planes = keep.tile([P, PACK, P], BF16, name="w_planes")
         nc.sync.dma_start(out=w_planes[:], in_=w_q.rearrange("(p t) c -> p t c", t=PACK))
-        load_x(3)
         small = {}
         for name, matrix in (
             ("mc", multichain_mask_2d), ("ux", unit_x), ("uy", unit_y), ("uz", unit_z),
@@ -282,6 +289,7 @@ def tile_templatepairembeddermultimer_pa_kernel(
         ):
             small[name] = keep.tile([P, P], BF16, name="in_" + name)
             nc.sync.dma_start(out=small[name][:], in_=matrix)
+        load_x(3)
 
         for s in range(LAG_TRANSPOSE):
             step(s)

from contextlib import ExitStack

import concourse.mybir as mybir
from concourse.masks import make_identity

F32 = mybir.dt.float32
BF16 = mybir.dt.bfloat16
U32 = mybir.dt.uint32
U8 = mybir.dt.uint8
FP8X4 = mybir.dt.float8_e4m3fn_x4
ALU = mybir.AluOpType
ACT = mybir.ActivationFunctionType

P = 128
C_IN = 512
PACK = 4
LN_EPS = 1e-5
GROUP = 4
PAIRS = GROUP * P
N_GROUPS = P // GROUP
N_FEAT = 5
GPSIMD_PAIRS = 7 * PAIRS // 8
X_AHEAD = 4

ROW_W = 0
ROW_PBM = 5
ROW_BBM = 6
ROW_BIAS = 7
N_ROWS = 13

STACK_COLUMNS = 8
STACK_ROWS = STACK_COLUMNS * N_FEAT
FIRST_STACKS = N_GROUPS // STACK_COLUMNS
ODD_STACKS = N_GROUPS // 2 // STACK_COLUMNS
N_STACKS = FIRST_STACKS + ODD_STACKS + 1
EXTRA_EVERY = 8
EXTRA_GROUPS = range(EXTRA_EVERY, N_GROUPS, EXTRA_EVERY)


def matmul_columns(g):
    return 2 if g % 2 == 1 or g in EXTRA_GROUPS else 1


def products_step(g):
    return g + (LAG_REGROUP if g < N_GROUPS // 2 else LAG_TRANSPOSE)


def place_in_stack(g, jj):
    if jj == 0:
        return divmod(g, STACK_COLUMNS)
    if g % 2 == 1:
        tile, local = divmod(g // 2, STACK_COLUMNS)
        return FIRST_STACKS + tile, local
    return N_STACKS - 1, EXTRA_GROUPS.index(g)


LAG_NORMALISE = 1
LAG_TRANSPOSE = 2
LAG_REGROUP = 3
LAG_PROJECT = 4
LAG_TURN_BACK = 5
N_STEPS = N_GROUPS + LAG_TURN_BACK
FIRST_LATE_GROUP = N_GROUPS - LAG_REGROUP

FLOPS = 2 * P * P * C_IN * P


def as_row(vector):
    return vector.rearrange("(o c) -> o c", o=1)


def tile_templatepairembeddermultimer_pa_kernel(
    tc,
    act_dgram, aa_proj1, aa_proj2, esm_proj1, esm_proj2, query_embedding,
    pseudo_beta_mask, backbone_mask, multichain_mask_2d, unit_x, unit_y, unit_z,
    ln_g, ln_b, w_q, b_q, w_pbm, b_pbm, w_x, b_x, w_y, b_y, w_z, b_z, w_bb, b_bb,
    out,
):
    nc = tc.nc
    with ExitStack() as stack:
        stack.enter_context(tc.manual_schedule())
        keep = stack.enter_context(tc.tile_pool(name="keep", bufs=1))
        x_pool = stack.enter_context(tc.tile_pool(name="x", bufs=X_AHEAD + LAG_NORMALISE + 1))
        act_pool = stack.enter_context(tc.tile_pool(name="act", bufs=LAG_TURN_BACK + 2))
        stat_pool = stack.enter_context(tc.tile_pool(name="stat", bufs=4))
        work = stack.enter_context(tc.tile_pool(name="work", bufs=3))
        psum_y = stack.enter_context(tc.psum_pool(name="psum_y", bufs=PACK))

        x_tiles, act_tiles, stats, rstds, y_tiles, y_banks, plane_tiles = {}, {}, {}, {}, {}, {}, {}
        product_tiles, term_banks, term_tiles = {}, {}, {}
        partials, grouped_tiles, code_tiles, proj_banks, proj_tiles, bases = {}, {}, {}, {}, {}, {}

        def columns_of(g):
            return slice(g * GROUP, (g + 1) * GROUP)

        def load_x(g):
            x_tiles[g] = x_pool.tile([P, GROUP, C_IN], BF16, name="x_g")
            nc.sync.dma_start(out=x_tiles[g][:], in_=query_embedding[:, columns_of(g), :])

        def load_act(g):
            act_tiles[g] = act_pool.tile([P, GROUP, P], BF16, name="act_g")
            nc.sync.dma_start(out=act_tiles[g][:], in_=act_dgram[:, columns_of(g), :])

        def bn_stats(g, jj):
            if jj == 0:
                stats[g] = stat_pool.tile([P, GROUP, 2], F32, name="stats")
                partials[g] = stat_pool.tile([P, GROUP, 6], F32, name="partials")
            nc.vector.bn_stats(out=partials[g][:, jj, :], in_=x_tiles[g][:, jj, :])

        def bn_aggr(g, jj):
            nc.vector.bn_aggr(out=stats[g][:, jj, :], in_=partials[g][:, jj, :])

        def inverse_std(g):
            rstds[g] = stat_pool.tile([P, GROUP], F32, name="rstd")
            nc.scalar.activation(
                out=rstds[g][:], in_=stats[g][:, :, 1], func=ACT.Abs_reciprocal_sqrt, bias=eps[:, 0:1], scale=1.0)

        def normalise(g):
            y_tiles[g] = work.tile([P, GROUP, PACK, P], F32, name="y_g")
            for jj in range(GROUP):
                nc.vector.tensor_scalar(
                    out=y_tiles[g][:, jj, :, :], in0=x_tiles[g][:, jj, :].rearrange("i (p t) -> i t p", t=PACK),
                    scalar1=stats[g][:, jj, 0:1], scalar2=rstds[g][:, jj : jj + 1], op0=ALU.subtract, op1=ALU.mult)

        def transpose(g):
            y_banks[g] = []
            for t in range(PACK):
                y_t = psum_y.tile([P, GROUP, P], F32, name="y_t")
                for jj in range(GROUP):
                    nc.tensor.transpose(y_t[:, jj, :], y_tiles[g][:, jj, t, :], ident_f[:])
                y_banks[g].append(y_t)

        def gain_shift(g, t):
            if t == 0:
                plane_tiles[g] = work.tile([P, PACK, PAIRS], BF16, name="q_planes")
            nc.scalar.activation(
                out=plane_tiles[g][:, t, :], in_=y_banks[g][t][:].rearrange("p a b -> p (a b)"), func=ACT.Identity,
                scale=gain[:, t : t + 1], bias=shift[:, t : t + 1])

        def regroup(g):
            grouped_tiles[g] = work.tile([P, PAIRS, PACK], BF16, name="q_grouped", align_bytes=64)
            planes = plane_tiles[g][:].rearrange("p t r -> p r t")
            if g < FIRST_LATE_GROUP:
                n = GPSIMD_PAIRS
                nc.vector.tensor_copy(out=grouped_tiles[g][:, n - PACK :, :], in_=planes[:, n - PACK :, :])
                nc.gpsimd.tensor_scalar(
                    out=grouped_tiles[g][:, 0:n, :], in0=planes[:, 0:n, :],
                    scalar1=1.0, scalar2=0.0, op0=ALU.mult, op1=ALU.add)
            else:
                nc.vector.tensor_copy(out=grouped_tiles[g][:], in_=planes)

        def quantise(g):
            q_codes = work.tile([P, PAIRS], U32, name="q_codes", align_bytes=64)
            q_scales = work.tile([P, PAIRS], U8, name="q_scales", align_bytes=64)
            nc.vector.quantize_mx(
                out=q_codes[:].bitcast(FP8X4), scales=q_scales[:], in_=grouped_tiles[g][:].rearrange("p r t -> p (r t)"))
            code_tiles[g] = (q_codes, q_scales)

        def project(g):
            q_codes, q_scales = code_tiles[g]
            proj_banks[g] = psum_mx.tile([P, PAIRS], F32, name="proj_ps")
            nc.tensor.matmul_mx(
                out=proj_banks[g][:],
                lhsT=w_codes[:].bitcast(FP8X4), lhsT_scale=w_scales[:],
                rhs=q_codes[:].bitcast(FP8X4), rhs_scale=q_scales[:],
                start=True, stop=True)

        def copy_out(g):
            proj_tiles[g] = work.tile([P, GROUP, P], F32, name="proj_t")
            nc.scalar.copy(out=proj_tiles[g][:].rearrange("p a b -> p (a b)"), in_=proj_banks[g][:])

        def other_columns(g):
            return range(matmul_columns(g), GROUP)

        def products(g, jj):
            if jj == matmul_columns(g):
                product_tiles[g] = work.tile([P, GROUP, N_FEAT, P], F32, name="products")
            j = g * GROUP + jj
            for m in range(N_FEAT):
                nc.scalar.activation(
                    out=product_tiles[g][:, jj, m, :], in_=w_spread[:, m, :], func=ACT.Copy, scale=feat[:, m, j : j + 1])

        def add_up(g):
            term_banks[g] = psum_terms.tile([P, GROUP, P], F32, name="term_ps")
            for jj in other_columns(g):
                for m in range(N_FEAT):
                    nc.tensor.matmul(
                        out=term_banks[g][:, jj, :], lhsT=product_tiles[g][:, jj, m, :], rhs=ident_f[:],
                        is_transpose=True, start=m == 0, stop=m == N_FEAT - 1)

        def copy_terms(g):
            term_tiles[g] = work.tile([P, GROUP, P], F32, name="term_t")
            n = matmul_columns(g)
            nc.scalar.copy(out=term_tiles[g][:, n:, :], in_=term_banks[g][:, n:, :])

        def turn_back(g):
            base = psum_base.tile([P, GROUP, P], F32, name="base")
            bases[g] = base
            for jj in range(GROUP):
                j = g * GROUP + jj
                by_matmul = jj < matmul_columns(g)
                if by_matmul:
                    tile, local = place_in_stack(g, jj)
                    nc.tensor.matmul(out=base[:, jj, :], lhsT=feat_stacks[:, tile, :], rhs=w_blocks[:, local, :],
                                     start=True, stop=False)
                nc.tensor.matmul(out=base[:, jj, :], lhsT=col_term_t[:], rhs=ident_f[:], is_transpose=True,
                                 start=not by_matmul, stop=False)
                nc.tensor.matmul(out=base[:, jj, :], lhsT=row_term_t[:, j : j + 1].to_broadcast([P, P]), rhs=ident_f[:],
                                 is_transpose=True, start=False, stop=False)
                if not by_matmul:
                    nc.tensor.matmul(out=base[:, jj, :], lhsT=term_tiles[g][:, jj, :], rhs=ident_f[:], is_transpose=True,
                                     start=False, stop=False)
                nc.tensor.matmul(out=base[:, jj, :], lhsT=proj_tiles[g][:, jj, :], rhs=ident_f[:], is_transpose=True,
                                 start=False, stop=True)

        def add_store(g):
            res = work.tile([P, GROUP, P], F32, name="res")
            nc.vector.tensor_tensor(out=res[:], in0=act_tiles[g][:], in1=bases[g][:], op=ALU.add)
            nc.sync.dma_start(out=out[:, columns_of(g), :], in_=res[:])

        def in_range(g):
            return 0 <= g < N_GROUPS

        def step(s):
            def run(calls):
                for call, g, *rest in calls:
                    if in_range(g):
                        call(g, *rest)

            normalised, turned, regrouped = s - LAG_NORMALISE, s - LAG_TRANSPOSE, s - LAG_REGROUP
            projected, back = s - LAG_PROJECT, s - LAG_TURN_BACK
            run([(load_x, s + X_AHEAD), (load_act, s)])
            run([(transpose, turned), (add_up, projected), (turn_back, back)])
            if s > LAG_TRANSPOSE:
                run([(inverse_std, normalised)])
            for t in range(PACK):
                for g in (regrouped, turned):
                    if in_range(g) and s == products_step(g) and t in other_columns(g):
                        products(g, t)
                run([(gain_shift, turned, t)])
            if s <= LAG_TRANSPOSE:
                run([(inverse_std, normalised)])
            run([(copy_terms, projected)])
            statistics = [(bn_stats, s, jj) for jj in range(GROUP)] + [(bn_aggr, s, jj) for jj in range(GROUP)]
            if s < LAG_TRANSPOSE:
                run([(normalise, normalised)] + statistics)
            else:
                run(statistics + [(quantise, projected), (normalise, normalised)])
            run([(regroup, regrouped), (add_store, back)])
            run([(project, projected)])
            run([(copy_out, projected)])

        eps = keep.tile([P, 1], F32, name="eps")
        nc.vector.memset(eps[:], LN_EPS)
        rows = keep.tile([P, P], BF16, name="rows")
        nc.vector.memset(rows[:], 0.0)
        table_warm = keep.tile([P, 1], F32, name="table_warm")
        nc.scalar.activation(out=table_warm[:], in_=eps[:], func=ACT.Abs_reciprocal_sqrt)
        ident_f = keep.tile([P, P], F32, name="ident_f")
        make_identity(nc, ident_f[:])
        ident_b = keep.tile([P, P], BF16, name="ident_b")
        make_identity(nc, ident_b[:])
        same_column = keep.tile([P, STACK_COLUMNS], F32, name="same_column")
        nc.vector.reduce_sum(
            out=same_column[:], in_=ident_f[:, 0:STACK_ROWS].rearrange("p (l m) -> p l m", m=N_FEAT),
            axis=mybir.AxisListType.X)
        w_stack_t = keep.tile([P, P], F32, name="w_stack_t")
        nc.gpsimd.memset(w_stack_t[:], 0.0)
        feat_cols = keep.tile([P, N_STACKS, P], F32, name="feat_cols")
        nc.gpsimd.memset(feat_cols[:], 0.0)

        load_x(0)
        load_x(1)
        gain_in = keep.tile([P, PACK], BF16, name="gain_in")
        nc.sync.dma_start(out=gain_in[:], in_=ln_g.rearrange("(p t) -> p t", t=PACK))
        shift_in = keep.tile([P, PACK], BF16, name="shift_in")
        nc.sync.dma_start(out=shift_in[:], in_=ln_b.rearrange("(p t) -> p t", t=PACK))
        for n, row in enumerate((w_pbm, w_x, w_y, w_z, w_bb, as_row(pseudo_beta_mask), as_row(backbone_mask))):
            nc.sync.dma_start(out=rows[ROW_W + n : ROW_W + n + 1, :], in_=row)
        for n, vector in enumerate((b_q, b_pbm, b_x, b_y, b_z, b_bb)):
            nc.sync.dma_start(out=rows[ROW_BIAS + n : ROW_BIAS + n + 1, :], in_=as_row(vector))
        load_x(2)
        w_planes = keep.tile([P, PACK, P], BF16, name="w_planes")
        nc.sync.dma_start(out=w_planes[:], in_=w_q.rearrange("(p t) c -> p t c", t=PACK))
        small = {}
        for name, matrix in (
            ("mc", multichain_mask_2d), ("ux", unit_x), ("uy", unit_y), ("uz", unit_z),
            ("aa1", aa_proj1), ("esm1", esm_proj1), ("aa2", aa_proj2), ("esm2", esm_proj2),
        ):
            small[name] = keep.tile([P, P], BF16, name="in_" + name)
            nc.sync.dma_start(out=small[name][:], in_=matrix)
        load_x(3)

        for s in range(LAG_TRANSPOSE):
            step(s)
        gain = keep.tile([P, PACK], F32, name="gain")
        nc.scalar.copy(out=gain[:], in_=gain_in[:])
        shift = keep.tile([P, PACK], F32, name="shift")
        nc.scalar.copy(out=shift[:], in_=shift_in[:])

        columns = keep.tile([P, N_ROWS], F32, name="columns")
        bias_total = keep.tile([P, 1], F32, name="bias_total")
        row_term_t = keep.tile([P, P], F32, name="row_term_t")
        col_term_t = keep.tile([P, P], F32, name="col_term_t")
        feat = keep.tile([P, N_FEAT, P], F32, name="feat")
        w_spread = keep.tile([P, N_FEAT, P], F32, name="w_spread")

        def spread(dst, row):
            nc.tensor.transpose(dst, columns[:, row : row + 1].to_broadcast([P, P]), ident_f[:])

        with tc.psum_pool(name="psum_setup", bufs=1) as psum_setup:
            spread_a = psum_setup.tile([P, 4, P], F32, name="spread_a")
            spread_b = psum_setup.tile([P, 4, P], F32, name="spread_b")
            rows_t = psum_setup.tile([P, P], BF16, name="rows_t")
            nc.tensor.transpose(rows_t[:], rows[:], ident_b[:])
            nc.scalar.copy(out=columns[:], in_=rows_t[:, 0:N_ROWS])
            step(LAG_TRANSPOSE)

            w_grouped = keep.tile([P, P, PACK], BF16, name="w_grouped", align_bytes=64)
            nc.gpsimd.tensor_scalar(
                out=w_grouped[:], in0=w_planes[:].rearrange("p t c -> p c t"),
                scalar1=1.0, scalar2=0.0, op0=ALU.mult, op1=ALU.add)
            row_term = keep.tile([P, P], F32, name="row_term")
            nc.gpsimd.tensor_tensor(out=row_term[:], in0=small["aa1"][:], in1=small["esm1"][:], op=ALU.add)
            col_term = keep.tile([P, P], F32, name="col_term")
            nc.gpsimd.tensor_tensor(out=col_term[:], in0=small["aa2"][:], in1=small["esm2"][:], op=ALU.add)

            nc.scalar.copy(
                out=w_stack_t[:, 0:STACK_ROWS].rearrange("p (l m) -> p l m", m=N_FEAT),
                in_=columns[:, ROW_W : ROW_W + N_FEAT].unsqueeze(1).to_broadcast([P, STACK_COLUMNS, N_FEAT]))
            nc.tensor.transpose(spread_b[:, 3, :], w_stack_t[:], ident_f[:])
            w_blocks = keep.tile([P, STACK_COLUMNS, P], F32, name="w_blocks")
            w_stack = keep.tile([P, P], F32, name="w_stack")
            nc.scalar.copy(out=w_stack[:], in_=spread_b[:, 3, :])
            nc.gpsimd.tensor_tensor(
                out=w_blocks[:], in0=w_stack[:].unsqueeze(1).to_broadcast([P, STACK_COLUMNS, P]),
                in1=same_column[:].unsqueeze(2).to_broadcast([P, STACK_COLUMNS, P]), op=ALU.mult)

            for m in range(4):
                spread(spread_a[:, m, :], ROW_W + m)
            spread(spread_b[:, 0, :], ROW_W + 4)
            spread(spread_b[:, 1, :], ROW_PBM)
            spread(spread_b[:, 2, :], ROW_BBM)
            nc.scalar.copy(out=w_spread[:, 0:4, :], in_=spread_a[:])
            nc.scalar.copy(out=w_spread[:, 4, :], in_=spread_b[:, 0, :])
            nc.vector.reduce_sum(out=bias_total[:], in_=columns[:, ROW_BIAS:N_ROWS], axis=mybir.AxisListType.X)

            w_codes = keep.tile([P, P], U32, name="w_codes", align_bytes=64)
            w_scales = keep.tile([P, P], U8, name="w_scales", align_bytes=64)
            nc.vector.quantize_mx(
                out=w_codes[:].bitcast(FP8X4), scales=w_scales[:], in_=w_grouped[:].rearrange("p c t -> p (c t)"))

            nc.vector.scalar_tensor_tensor(
                out=feat[:, 0, :], in0=small["mc"][:], scalar=columns[:, ROW_PBM : ROW_PBM + 1], in1=spread_b[:, 1, :],
                op0=ALU.mult, op1=ALU.mult)
            nc.vector.scalar_tensor_tensor(
                out=feat[:, 4, :], in0=small["mc"][:], scalar=columns[:, ROW_BBM : ROW_BBM + 1], in1=spread_b[:, 2, :],
                op0=ALU.mult, op1=ALU.mult)
            for m, name in ((1, "ux"), (2, "uy"), (3, "uz")):
                nc.vector.tensor_tensor(out=feat[:, m, :], in0=small[name][:], in1=feat[:, 4, :], op=ALU.mult)

            term_bank = psum_setup.tile([P, 4, P], F32, name="term_bank")
            nc.tensor.transpose(term_bank[:, 0, :], row_term[:], ident_f[:])
            nc.tensor.transpose(term_bank[:, 1, :], col_term[:], ident_f[:])
            nc.scalar.copy(out=row_term_t[:], in_=term_bank[:, 0, :])
            nc.scalar.activation(
                out=col_term_t[:], in_=term_bank[:, 1, :], func=ACT.Identity, bias=bias_total[:, 0:1], scale=1.0)

            feat_stacks = keep.tile([P, N_STACKS, P], F32, name="feat_stacks")
            for first, last, j0, j_step in (
                (0, FIRST_STACKS, 0, GROUP),
                (FIRST_STACKS, N_STACKS - 1, GROUP + 1, 2 * GROUP),
                (N_STACKS - 1, N_STACKS, EXTRA_EVERY * GROUP + 1, EXTRA_EVERY * GROUP),
            ):
                for n in range(first, last):
                    j = j0 + (n - first) * STACK_COLUMNS * j_step
                    n_columns = len(range(j, P, j_step)[:STACK_COLUMNS])
                    nc.gpsimd.tensor_scalar(
                        out=feat_cols[:, n, 0 : n_columns * N_FEAT].rearrange("p (l m) -> p m l", m=N_FEAT),
                        in0=feat[:, :, j : j + (n_columns - 1) * j_step + 1 : j_step],
                        scalar1=1.0, scalar2=0.0, op0=ALU.mult, op1=ALU.add)
            step(LAG_REGROUP)
            banks = [spread_a[:, 0:4, :], term_bank[:, 2:4, :], spread_b[:, 3:4, :]]
            for n0, bank in zip((0, 4, 6), banks):
                for n in range(bank.shape[1]):
                    nc.tensor.transpose(bank[:, n, :], feat_cols[:, n0 + n, :], ident_f[:])
                nc.vector.tensor_copy(out=feat_stacks[:, n0 : n0 + bank.shape[1], :], in_=bank)

        psum_mx = stack.enter_context(tc.psum_pool(name="psum_mx", bufs=1))
        psum_terms = stack.enter_context(tc.psum_pool(name="psum_terms", bufs=1))
        psum_base = stack.enter_context(tc.psum_pool(name="psum_base", bufs=2))

        for s in range(LAG_PROJECT, N_STEPS):
            step(s)
